import numpy as np
import ml_dtypes


def mxq(x, axis, fmt="e4m3"):
    dtype, down = {"e4m3": (ml_dtypes.float8_e4m3fn, 7), "e5m2": (ml_dtypes.float8_e5m2, 14)}[fmt]
    v = np.moveaxis(np.asarray(x, np.float32).astype(ml_dtypes.bfloat16).astype(np.float64), axis, -1)
    blocks = v.reshape(v.shape[:-1] + (-1, 32))
    amax = np.abs(blocks).max(-1, keepdims=True)
    byte = np.maximum(np.where(amax > 0, np.frexp(amax)[1] - 1 + 127, 0) - down, 1)
    scale = np.exp2(byte - 127.0)
    codes = (blocks / scale).astype(np.float32).astype(dtype).astype(np.float64)
    return np.moveaxis((codes * scale).reshape(v.shape), -1, axis)


WIDE = False


def mx_kscale(k):
    if not WIDE:
        return np.ones(k)
    levels = np.array([10, -10, 5, -5, 0])
    a = np.random.permutation(np.resize(levels, k // 512 * 4)).reshape(k // 512, 4)
    idx = np.arange(k)
    return np.exp2(a[idx // 512, idx % 128 // 32])


BF16 = ml_dtypes.bfloat16


def bf(x):
    return np.asarray(x, np.float32).astype(BF16)


def f64(x):
    return np.asarray(x).astype(np.float64)


B, N, L, H, S, R, C = 4, 1024, 4, 64, 2, 2, 512


def setup_inputs():
    s = mx_kscale(N)
    return {"x": bf(np.random.standard_normal((B, N, L, H)) * s[None, :, None, None]),
            "support": bf(np.random.standard_normal((S, N, N)) * 0.6 / np.sqrt(N) * s[:, None] / s[None, :]),
            "eps": bf(np.random.uniform(0.1, 0.3, (1,)))}


def reference(x, support, eps):
    xv = f64(x).reshape(B, N, L * H)
    sup = f64(support)
    g = 1.0 + f64(eps)
    xq = mxq(xv, 1, "e4m3")
    res = []
    for i in range(S):
        aq = mxq(sup[i], 1, "e4m3")
        out, oq = xv, xq
        for j in range(R):
            out = g * out + (aq @ oq)
            res.append(out)
            if j + 1 < R:
                oq = mxq(out, 1, "e4m3")
    return np.stack(res, axis=-1).reshape(B, N, L, H * len(res))

@@ -1,0 +1,315 @@
+from contextlib import ExitStack
+
+import concourse.mybir as mybir
+from concourse.masks import make_identity
+
+F32 = mybir.dt.float32
+BF16 = mybir.dt.bfloat16
+U32 = mybir.dt.uint32
+U8 = mybir.dt.uint8
+FP8X4 = mybir.dt.float8_e4m3fn_x4
+MULT = mybir.AluOpType.mult
+ADD = mybir.AluOpType.add
+
+P = 128
+B = 4
+D = 256
+S = 2
+NT = 8
+FLOPS = 4 * 2 * 1024 * 1024 * 1024
+
+MANUAL = False
+DEFER_H = 2
+PRE = 1
+X_ENG = ["v", "g", "g", "g"]
+R_ENG = {0: ["s", "s"], 1: ["s", "g"]}
+ILV = ["s", "g", "s", "s", "g", "s", "g", "s"]
+ILV_FIRST = ["s", "v", "s", "g", "s", "g", "s", "g"]
+ILV_LAST = ["s", "g", "s", "g", "s", "g", "s", "v"]
+E_LAST = ["s", "s"]
+XR3_AT = 1
+XQ2_AT = 0
+XQ3_AT = 3
+RATES = [1, 1, 1, 1, 1, 1, 1, 1, 1, 1, 1, 1, 0, 0, 0, 0]
+HH_BUFS = 6
+O_BUFS = 4
+
+
+def tile_ginconvfft_pa_t_kernel(tc, x, support, eps, out):
+    nc = tc.nc
+    with ExitStack() as ctx:
+        keep = ctx.enter_context(tc.tile_pool(name="keep", bufs=1))
+        atg_pool = ctx.enter_context(tc.tile_pool(name="atg", bufs=4))
+        xg_pool = ctx.enter_context(tc.tile_pool(name="xg", bufs=2))
+        hh_pool = ctx.enter_context(tc.tile_pool(name="hh", bufs=HH_BUFS))
+        hg_pool = ctx.enter_context(tc.tile_pool(name="hg", bufs=3))
+        hc_pool = ctx.enter_context(tc.tile_pool(name="hc", bufs=6))
+        o_pool = ctx.enter_context(tc.tile_pool(name="o", bufs=O_BUFS))
+        psum = ctx.enter_context(tc.psum_pool(name="psum", bufs=8))
+        if MANUAL:
+            ctx.enter_context(tc.manual_schedule())
+
+        def copy(eng, dst, src):
+            if eng == "v":
+                nc.vector.tensor_copy(out=dst, in_=src)
+            elif eng == "s":
+                nc.scalar.copy(out=dst, in_=src)
+            else:
+                nc.gpsimd.tensor_scalar(out=dst, in0=src, scalar1=1.0, scalar2=0.0, op0=MULT, op1=ADD)
+
+        ident = keep.tile([P, P], F32, name="ident")
+        make_identity(nc, ident[:])
+        eps_sb = keep.tile([P, 1], BF16, name="eps_sb")
+        nc.scalar.dma_start(out=eps_sb[:], in_=eps.partition_broadcast(P))
+        gain = keep.tile([P, 1], F32, name="gain")
+        nc.vector.tensor_scalar_add(out=gain[:], in0=eps_sb[:], scalar1=1.0)
+
+        x_raw = {}
+        a_raw = {}
+
+        def load_x(b):
+            t = keep.tile([P, NT, D], BF16, name="x_raw%d" % b)
+            nc.sync.dma_start(
+                out=t[:].rearrange("p (q e) d -> p q (e d)", e=2),
+                in_=x[b].rearrange("(q p e) l h -> p q (e l h)", q=4, p=P, e=2),
+            )
+            x_raw[b] = t
+
+        def load_a(s, gu):
+            if (gu // 2) not in a_raw:
+                a_raw[gu // 2] = hh_pool.tile([P, 4, 2048], BF16, name="a_raw", tag="hh")
+            nc.sync.dma_start(
+                out=a_raw[gu // 2][:, 2 * (gu % 2) + s, :],
+                in_=support[s, 256 * gu : 256 * (gu + 1), :].rearrange("(p e) m -> p (e m)", e=2),
+            )
+
+        load_x(0)
+        for gu in range(4):
+            for s in range(S):
+                load_a(s, gu)
+        for b in range(1, B):
+            load_x(b)
+
+        x_grp = {}
+        x_codes = {}
+        x_scales = {}
+
+        def regroup_x(b):
+            t = xg_pool.tile([P, 2, D, 4], BF16, name="x_grp", align_bytes=64)
+            copy(X_ENG[b], t[:], x_raw[b][:].rearrange("p (g t) d -> p g d t", t=4))
+            x_grp[b] = t
+
+        def quant_x(b):
+            c = keep.tile([P, 512], U32, name="x_codes%d" % b, align_bytes=64)
+            sc = keep.tile([P, 512], U8, name="x_scales%d" % b, align_bytes=64)
+            nc.vector.quantize_mx(
+                out=c[:].bitcast(FP8X4), scales=sc[:], in_=x_grp[b][:].rearrange("p g d t -> p (g d t)")
+            )
+            x_codes[b] = c
+            x_scales[b] = sc
+
+        at_grp = {}
+        at_codes = {}
+        at_scales = {}
+
+        def transpose_a(s, gu, engs):
+            a32 = a_raw[gu // 2][:, 2 * (gu % 2) + s, :].bitcast(F32)
+            grp = atg_pool.tile([P, 2048], BF16, name="at_grp", align_bytes=64)
+            g32 = grp[:].bitcast(F32)
+            banks = []
+            for g in range(2):
+                bank = psum.tile([P, 512], F32, name="bank", tag="bank")
+                for u in range(2):
+                    for e in range(2):
+                        w0 = 512 * e + 256 * g + 128 * u
+                        nc.tensor.transpose(
+                            out=bank[:, 256 * u + 128 * e : 256 * u + 128 * (e + 1)],
+                            in_=a32[:, w0 : w0 + 128],
+                            identity=ident[:],
+                        )
+                banks.append(bank)
+            for g in range(2):
+                copy(
+                    engs[g],
+                    g32[:, 512 * g : 512 * (g + 1)].rearrange("p (w u) -> p w u", u=2),
+                    banks[g][:].rearrange("p (u w) -> p w u", u=2),
+                )
+            at_grp[(s, gu)] = grp
+
+        def quant_a(s, gu):
+            c = keep.tile([P, 512], U32, name="at_codes%d_%d" % (s, gu), align_bytes=64)
+            sc = keep.tile([P, 512], U8, name="at_scales%d_%d" % (s, gu), align_bytes=64)
+            nc.vector.quantize_mx(out=c[:].bitcast(FP8X4), scales=sc[:], in_=at_grp[(s, gu)][:])
+            at_codes[(s, gu)] = c
+            at_scales[(s, gu)] = sc
+
+        state = {"later": []}
+
+        def defer(n, fn):
+            state["later"] = state["later"] + [[n, fn]]
+
+        def tick():
+            keep_l = []
+            for n, fn in state["later"]:
+                if n <= 1:
+                    fn()
+                else:
+                    keep_l.append([n - 1, fn])
+            state["later"] = keep_l
+
+        hh = {}
+        h_codes = {}
+        h_scales = {}
+
+        def mx_bank(nt, rhs_of):
+            gu, e = nt // 2, nt % 2
+            bank = psum.tile([P, 512], F32, name="bank", tag="bank")
+            for s in range(S):
+                for g in range(2):
+                    cols = slice(256 * g + 128 * e, 256 * g + 128 * (e + 1))
+                    rc, rs = rhs_of(s, g)
+                    nc.tensor.matmul_mx(
+                        out=bank[:, D * s : D * (s + 1)],
+                        lhsT=at_codes[(s, gu)][:, cols].bitcast(FP8X4),
+                        lhsT_scale=at_scales[(s, gu)][:, cols],
+                        rhs=rc.bitcast(FP8X4),
+                        rhs_scale=rs,
+                        start=(g == 0),
+                        stop=(g == 1),
+                    )
+            return bank
+
+        def quant_h(b, g, grp):
+            c = hc_pool.tile([P, 512], U32, name="h_codes", align_bytes=64)
+            sc = hc_pool.tile([P, 512], U8, name="h_scales", align_bytes=64)
+            nc.vector.quantize_mx(out=c[:].bitcast(FP8X4), scales=sc[:], in_=grp[:].rearrange("p s c t -> p (s c t)"))
+            h_codes[(b, g)] = c
+            h_scales[(b, g)] = sc
+
+        def hop1_mm(b, nt):
+            return mx_bank(nt, lambda s, gk: (x_codes[b][:, D * gk : D * (gk + 1)], x_scales[b][:, D * gk : D * (gk + 1)]))
+
+        def hop1_add(b, nt, bank):
+            g, t = nt // 4, nt % 4
+            if t == 0:
+                hh[(b, g)] = hh_pool.tile([P, 4, 2, D, S], F32, name="hh", tag="hh")
+            tl = hh[(b, g)]
+            nc.vector.scalar_tensor_tensor(
+                out=tl[:, t, 0, :, :],
+                in0=x_raw[b][:, nt, :].unsqueeze(2).to_broadcast([P, D, S]),
+                scalar=gain[:, 0:1],
+                in1=bank[:].rearrange("p (s c) -> p c s", s=S),
+                op0=MULT,
+                op1=ADD,
+            )
+            tick()
+            if t == 3 and b > 0:
+                grp = regroup_h(b, g, R_ENG[g])
+                defer(DEFER_H, lambda: quant_h(b, g, grp))
+
+        def regroup_h(b, g, engs):
+            grp = hg_pool.tile([P, S, D, 4], BF16, name="h_grp", align_bytes=64)
+            for s in range(S):
+                copy(engs[s], grp[:, s, :, :], hh[(b, g)][:, :, 0, :, s].rearrange("p t c -> p c t"))
+            return grp
+
+        def hop1_unit(b, gu):
+            banks = [hop1_mm(b, 2 * gu + e) for e in range(2)]
+            for e in range(2):
+                hop1_add(b, 2 * gu + e, banks[e])
+
+        def hop2_unit(b, gu, ilv):
+            banks = []
+            for e in range(2):
+                banks.append(
+                    mx_bank(
+                        2 * gu + e,
+                        lambda s, gk: (
+                            h_codes[(b, gk)][:, D * s : D * (s + 1)],
+                            h_scales[(b, gk)][:, D * s : D * (s + 1)],
+                        ),
+                    )
+                )
+            o = o_pool.tile([P, 2, 4 * D], F32, name="o")
+            tl = hh[(b, gu // 2)]
+            for e in range(2):
+                t = (2 * gu + e) % 4
+                nc.vector.scalar_tensor_tensor(
+                    out=tl[:, t, 1, :, :],
+                    in0=tl[:, t, 0, :, :],
+                    scalar=gain[:, 0:1],
+                    in1=banks[e][:].rearrange("p (s c) -> p c s", s=S),
+                    op0=MULT,
+                    op1=ADD,
+                )
+                tick()
+            for e in range(2):
+                t = (2 * gu + e) % 4
+                copy(
+                    ilv[2 * gu + e],
+                    o[:, e, :].rearrange("p (f j) -> p f j", j=2),
+                    tl[:, t, :, :, :].rearrange("p j c s -> p (c s) j"),
+                )
+            nc.sync.dma_start(
+                out=out[b, 256 * gu : 256 * (gu + 1)].rearrange("(p e) l f -> p (e l f)", e=2),
+                in_=o[:].rearrange("p e f -> p (e f)"),
+            )
+
+        regroup_x(0)
+        quant_x(0)
+        bank_of = {}
+
+        def mm(nts):
+            for nt in nts:
+                bank_of[nt] = hop1_mm(0, nt)
+
+        def add(nts):
+            for nt in nts:
+                hop1_add(0, nt, bank_of[nt])
+
+        for gu in range(2):
+            for s in range(S):
+                transpose_a(s, gu, ["s", "s"])
+                quant_a(s, gu)
+        mm([0, 1])
+        transpose_a(0, 2, ["s", "s"])
+        transpose_a(1, 2, ["s", "s"])
+        add([0, 1])
+        quant_a(0, 2)
+        quant_a(1, 2)
+        mm([2])
+        transpose_a(0, 3, ["s", "s"])
+        transpose_a(1, 3, E_LAST)
+        regroup_x(1)
+        add([2])
+        mm([3, 4, 5])
+        add([3])
+        grp00 = regroup_h(0, 0, ["s", "s"])
+        quant_a(0, 3)
+        add([4])
+        quant_a(1, 3)
+        add([5])
+        mm([6, 7])
+        add([6, 7])
+        grp01 = regroup_h(0, 1, ["s", "g"])
+        quant_h(0, 0, grp00)
+        quant_x(1)
+        quant_h(0, 1, grp01)
+        regroup_x(2)
+
+        ones = [(b, gu) for b in range(1, B) for gu in range(4)]
+        twos = [(b, gu) for b in range(B) for gu in range(4)]
+        for b, gu in ones[:PRE]:
+            hop1_unit(b, gu)
+        ones = ones[PRE:]
+        for i, (b, gu) in enumerate(twos):
+            hop2_unit(b, gu, ILV_FIRST if b == 0 else (ILV_LAST if b == B - 1 else ILV))
+            if i == XR3_AT:
+                regroup_x(3)
+            if i == XQ2_AT:
+                quant_x(2)
+            if i == XQ3_AT:
+                quant_x(3)
+            for b1, gu1 in ones[: RATES[i]]:
+                hop1_unit(b1, gu1)
+            ones = ones[RATES[i] :]

@@ -21,11 +21,11 @@ FLOPS = 4 * 2 * 1024 * 1024 * 1024
 MANUAL = False
 DEFER_H = 2
 PRE = 1
-X_ENG = ["v", "g", "g", "g"]
-R_ENG = {0: ["s", "s"], 1: ["s", "g"]}
-ILV = ["s", "g", "s", "s", "g", "s", "g", "s"]
-ILV_FIRST = ["s", "v", "s", "g", "s", "g", "s", "g"]
-ILV_LAST = ["s", "g", "s", "g", "s", "g", "s", "v"]
+X_ENG = ["v", "s", "s", "s"]
+R_ENG = {0: ["s", "s"], 1: ["s", "s"]}
+ILV = ["s", "v", "s", "v", "s", "s", "v", "s"]
+ILV_FIRST = ["s", "v", "s", "v", "s", "s", "v", "s"]
+ILV_LAST = ["s", "v", "s", "v", "s", "v", "s", "v"]
 E_LAST = ["s", "s"]
 XR3_AT = 1
 XQ2_AT = 0
@@ -291,7 +291,7 @@ def tile_ginconvfft_pa_t_kernel(tc, x, support, eps, out):
         add([5])
         mm([6, 7])
         add([6, 7])
-        grp01 = regroup_h(0, 1, ["s", "g"])
+        grp01 = regroup_h(0, 1, ["s", "v"])
         quant_h(0, 0, grp00)
         quant_x(1)
         quant_h(0, 1, grp01)

@@ -22,15 +22,18 @@ MANUAL = False
 DEFER_H = 2
 PRE = 1
 X_ENG = ["v", "s", "s", "s"]
-R_ENG = {0: ["s", "s"], 1: ["s", "s"]}
-ILV = ["s", "v", "s", "v", "s", "s", "v", "s"]
-ILV_FIRST = ["s", "v", "s", "v", "s", "s", "v", "s"]
-ILV_LAST = ["s", "v", "s", "v", "s", "v", "s", "v"]
+R_ENG = ["ss", "ss", "ss", "ss", "ss", "ss", "ss", "vs"]
+ILV = ["gg", "gs", "sg", "sg", "gs", "ss", "gs", "sg", "gg", "sg", "gs", "sg", "sv", "gs", "vg", "vv"]
+E_ENG = ["sv", "ss", "vs", "ss", "sv", "ss", "ss", "sv"]
+G_SPLIT = 1
+X_FIRST = 1
+XG_BUFS = 2
+SPLIT_STORES = 0
 E_LAST = ["s", "s"]
-XR3_AT = 1
+XR3_AT = 0
 XQ2_AT = 0
-XQ3_AT = 3
-RATES = [1, 1, 1, 1, 1, 1, 1, 1, 1, 1, 1, 1, 0, 0, 0, 0]
+XQ3_AT = 5
+RATES = [1, 1, 1, 3, 0, 1, 1, 1, 1, 0, 1, 1, 0, 0, 0, 0]
 HH_BUFS = 6
 O_BUFS = 4
 
@@ -40,7 +43,7 @@ def tile_ginconvfft_pa_t_kernel(tc, x, support, eps, out):
     with ExitStack() as ctx:
         keep = ctx.enter_context(tc.tile_pool(name="keep", bufs=1))
         atg_pool = ctx.enter_context(tc.tile_pool(name="atg", bufs=4))
-        xg_pool = ctx.enter_context(tc.tile_pool(name="xg", bufs=2))
+        xg_pool = ctx.enter_context(tc.tile_pool(name="xg", bufs=XG_BUFS))
         hh_pool = ctx.enter_context(tc.tile_pool(name="hh", bufs=HH_BUFS))
         hg_pool = ctx.enter_context(tc.tile_pool(name="hg", bufs=3))
         hc_pool = ctx.enter_context(tc.tile_pool(name="hc", bufs=6))
@@ -55,7 +58,16 @@ def tile_ginconvfft_pa_t_kernel(tc, x, support, eps, out):
             elif eng == "s":
                 nc.scalar.copy(out=dst, in_=src)
             else:
-                nc.gpsimd.tensor_scalar(out=dst, in0=src, scalar1=1.0, scalar2=0.0, op0=MULT, op1=ADD)
+                n = dst.shape[1] // G_SPLIT
+                for i in range(G_SPLIT):
+                    nc.gpsimd.tensor_scalar(
+                        out=dst[:, i * n : (i + 1) * n],
+                        in0=src[:, i * n : (i + 1) * n],
+                        scalar1=1.0,
+                        scalar2=0.0,
+                        op0=MULT,
+                        op1=ADD,
+                    )
 
         ident = keep.tile([P, P], F32, name="ident")
         make_identity(nc, ident[:])
@@ -83,11 +95,12 @@ def tile_ginconvfft_pa_t_kernel(tc, x, support, eps, out):
                 in_=support[s, 256 * gu : 256 * (gu + 1), :].rearrange("(p e) m -> p (e m)", e=2),
             )
 
-        load_x(0)
+        for b in range(X_FIRST):
+            load_x(b)
         for gu in range(4):
             for s in range(S):
                 load_a(s, gu)
-        for b in range(1, B):
+        for b in range(X_FIRST, B):
             load_x(b)
 
         x_grp = {}
@@ -96,7 +109,8 @@ def tile_ginconvfft_pa_t_kernel(tc, x, support, eps, out):
 
         def regroup_x(b):
             t = xg_pool.tile([P, 2, D, 4], BF16, name="x_grp", align_bytes=64)
-            copy(X_ENG[b], t[:], x_raw[b][:].rearrange("p (g t) d -> p g d t", t=4))
+            for g in range(2):
+                copy(X_ENG[b], t[:, g, :, :], x_raw[b][:, 4 * g : 4 * (g + 1), :].rearrange("p t d -> p d t"))
             x_grp[b] = t
 
         def quant_x(b):
@@ -204,7 +218,7 @@ def tile_ginconvfft_pa_t_kernel(tc, x, support, eps, out):
             )
             tick()
             if t == 3 and b > 0:
-                grp = regroup_h(b, g, R_ENG[g])
+                grp = regroup_h(b, g, R_ENG[2 * b + g])
                 defer(DEFER_H, lambda: quant_h(b, g, grp))
 
         def regroup_h(b, g, engs):
@@ -218,7 +232,7 @@ def tile_ginconvfft_pa_t_kernel(tc, x, support, eps, out):
             for e in range(2):
                 hop1_add(b, 2 * gu + e, banks[e])
 
-        def hop2_unit(b, gu, ilv):
+        def hop2_unit(b, gu, ilv, split):
             banks = []
             for e in range(2):
                 banks.append(
@@ -246,17 +260,24 @@ def tile_ginconvfft_pa_t_kernel(tc, x, support, eps, out):
             for e in range(2):
                 t = (2 * gu + e) % 4
                 copy(
-                    ilv[2 * gu + e],
+                    ilv[e],
                     o[:, e, :].rearrange("p (f j) -> p f j", j=2),
                     tl[:, t, :, :, :].rearrange("p j c s -> p (c s) j"),
                 )
-            nc.sync.dma_start(
-                out=out[b, 256 * gu : 256 * (gu + 1)].rearrange("(p e) l f -> p (e l f)", e=2),
-                in_=o[:].rearrange("p e f -> p (e f)"),
-            )
+                if split:
+                    nc.sync.dma_start(
+                        out=out[b, 256 * gu : 256 * (gu + 1)].rearrange("(p e) l f -> p e (l f)", e=2)[:, e, :],
+                        in_=o[:, e, :],
+                    )
+            if not split:
+                nc.sync.dma_start(
+                    out=out[b, 256 * gu : 256 * (gu + 1)].rearrange("(p e) l f -> p (e l f)", e=2),
+                    in_=o[:].rearrange("p e f -> p (e f)"),
+                )
 
-        regroup_x(0)
-        quant_x(0)
+        for b in range(X_FIRST):
+            regroup_x(b)
+            quant_x(b)
         bank_of = {}
 
         def mm(nts):
@@ -269,33 +290,36 @@ def tile_ginconvfft_pa_t_kernel(tc, x, support, eps, out):
 
         for gu in range(2):
             for s in range(S):
-                transpose_a(s, gu, ["s", "s"])
+                transpose_a(s, gu, E_ENG[2 * gu + s])
                 quant_a(s, gu)
         mm([0, 1])
-        transpose_a(0, 2, ["s", "s"])
-        transpose_a(1, 2, ["s", "s"])
+        transpose_a(0, 2, E_ENG[4])
+        transpose_a(1, 2, E_ENG[5])
         add([0, 1])
         quant_a(0, 2)
         quant_a(1, 2)
         mm([2])
-        transpose_a(0, 3, ["s", "s"])
-        transpose_a(1, 3, E_LAST)
-        regroup_x(1)
+        transpose_a(0, 3, E_ENG[6])
+        transpose_a(1, 3, E_ENG[7])
+        if X_FIRST < 2:
+            regroup_x(1)
         add([2])
         mm([3, 4, 5])
         add([3])
-        grp00 = regroup_h(0, 0, ["s", "s"])
+        grp00 = regroup_h(0, 0, R_ENG[0])
         quant_a(0, 3)
         add([4])
         quant_a(1, 3)
         add([5])
         mm([6, 7])
         add([6, 7])
-        grp01 = regroup_h(0, 1, ["s", "v"])
+        grp01 = regroup_h(0, 1, R_ENG[1])
         quant_h(0, 0, grp00)
-        quant_x(1)
+        if X_FIRST < 2:
+            quant_x(1)
         quant_h(0, 1, grp01)
-        regroup_x(2)
+        if X_FIRST < 3:
+            regroup_x(2)
 
         ones = [(b, gu) for b in range(1, B) for gu in range(4)]
         twos = [(b, gu) for b in range(B) for gu in range(4)]
@@ -303,12 +327,12 @@ def tile_ginconvfft_pa_t_kernel(tc, x, support, eps, out):
             hop1_unit(b, gu)
         ones = ones[PRE:]
         for i, (b, gu) in enumerate(twos):
-            hop2_unit(b, gu, ILV_FIRST if b == 0 else (ILV_LAST if b == B - 1 else ILV))
-            if i == XR3_AT:
+            hop2_unit(b, gu, ILV[i], i >= len(twos) - SPLIT_STORES)
+            if i == XR3_AT and X_FIRST < 4:
                 regroup_x(3)
-            if i == XQ2_AT:
+            if i == XQ2_AT and X_FIRST < 3:
                 quant_x(2)
-            if i == XQ3_AT:
+            if i == XQ3_AT and X_FIRST < 4:
                 quant_x(3)
             for b1, gu1 in ones[: RATES[i]]:
                 hop1_unit(b1, gu1)

@@ -22,18 +22,19 @@ MANUAL = False
 DEFER_H = 2
 PRE = 1
 X_ENG = ["v", "s", "s", "s"]
-R_ENG = ["ss", "ss", "ss", "ss", "ss", "ss", "ss", "vs"]
-ILV = ["gg", "gs", "sg", "sg", "gs", "ss", "gs", "sg", "gg", "sg", "gs", "sg", "sv", "gs", "vg", "vv"]
-E_ENG = ["sv", "ss", "vs", "ss", "sv", "ss", "ss", "sv"]
+R_ENG = ["ss", "sg", "ss", "sg", "ss", "sg", "ss", "sg"]
+ILV = ["sg", "sg", "sg", "sg", "sg", "sg", "sg", "sg", "sg", "sg", "sg", "sg", "sg", "sg", "sg", "sv"]
+E_ENG = ["ss", "ss", "ss", "ss", "ss", "ss", "ss", "ss"]
 G_SPLIT = 1
 X_FIRST = 1
 XG_BUFS = 2
 SPLIT_STORES = 0
 E_LAST = ["s", "s"]
-XR3_AT = 0
+XR2_AT = -1
+XR3_AT = 1
 XQ2_AT = 0
-XQ3_AT = 5
-RATES = [1, 1, 1, 3, 0, 1, 1, 1, 1, 0, 1, 1, 0, 0, 0, 0]
+XQ3_AT = 3
+RATES = [1, 1, 1, 1, 1, 1, 1, 1, 1, 1, 1, 1, 0, 0, 0, 0]
 HH_BUFS = 6
 O_BUFS = 4
 
@@ -318,7 +319,7 @@ def tile_ginconvfft_pa_t_kernel(tc, x, support, eps, out):
         if X_FIRST < 2:
             quant_x(1)
         quant_h(0, 1, grp01)
-        if X_FIRST < 3:
+        if X_FIRST < 3 and XR2_AT < 0:
             regroup_x(2)
 
         ones = [(b, gu) for b in range(1, B) for gu in range(4)]
@@ -328,6 +329,8 @@ def tile_ginconvfft_pa_t_kernel(tc, x, support, eps, out):
         ones = ones[PRE:]
         for i, (b, gu) in enumerate(twos):
             hop2_unit(b, gu, ILV[i], i >= len(twos) - SPLIT_STORES)
+            if i == XR2_AT and X_FIRST < 3:
+                regroup_x(2)
             if i == XR3_AT and X_FIRST < 4:
                 regroup_x(3)
             if i == XQ2_AT and X_FIRST < 3:

@@ -19,32 +19,24 @@ NT = 8
 FLOPS = 4 * 2 * 1024 * 1024 * 1024
 
 MANUAL = False
-DEFER_H = 2
-PRE = 1
-X_ENG = ["v", "s", "s", "s"]
-R_ENG = ["ss", "sg", "ss", "sg", "ss", "sg", "ss", "sg"]
+DEFER_H = 4
+X_ENG = ["g", "s", "g", "g"]
+R_START = {(0, 0): "ss", (1, 0): "sg", (0, 1): "ss", (1, 1): "sg"}
+R_ENG = "ss"
+RATES = [1, 1, 1, 0, 1, 1, 1, 1, 1, 0, 0, 0, 0, 0, 0, 0]
 ILV = ["sg", "sg", "sg", "sg", "sg", "sg", "sg", "sg", "sg", "sg", "sg", "sg", "sg", "sg", "sg", "sv"]
-E_ENG = ["ss", "ss", "ss", "ss", "ss", "ss", "ss", "ss"]
-G_SPLIT = 1
-X_FIRST = 1
-XG_BUFS = 2
-SPLIT_STORES = 0
-E_LAST = ["s", "s"]
-XR2_AT = -1
-XR3_AT = 1
-XQ2_AT = 0
-XQ3_AT = 3
-RATES = [1, 1, 1, 1, 1, 1, 1, 1, 1, 1, 1, 1, 0, 0, 0, 0]
+G_SPLIT = 2
 HH_BUFS = 6
 O_BUFS = 4
+XQ_AT = {0: 2, 3: 3}
 
 
 def tile_ginconvfft_pa_t_kernel(tc, x, support, eps, out):
     nc = tc.nc
     with ExitStack() as ctx:
         keep = ctx.enter_context(tc.tile_pool(name="keep", bufs=1))
-        atg_pool = ctx.enter_context(tc.tile_pool(name="atg", bufs=4))
-        xg_pool = ctx.enter_context(tc.tile_pool(name="xg", bufs=XG_BUFS))
+        atg_pool = ctx.enter_context(tc.tile_pool(name="atg", bufs=2))
+        xg_pool = ctx.enter_context(tc.tile_pool(name="xg", bufs=2))
         hh_pool = ctx.enter_context(tc.tile_pool(name="hh", bufs=HH_BUFS))
         hg_pool = ctx.enter_context(tc.tile_pool(name="hg", bufs=3))
         hc_pool = ctx.enter_context(tc.tile_pool(name="hc", bufs=6))
@@ -96,30 +88,32 @@ def tile_ginconvfft_pa_t_kernel(tc, x, support, eps, out):
                 in_=support[s, 256 * gu : 256 * (gu + 1), :].rearrange("(p e) m -> p (e m)", e=2),
             )
 
-        for b in range(X_FIRST):
-            load_x(b)
+        load_x(0)
+        load_x(1)
         for gu in range(4):
             for s in range(S):
                 load_a(s, gu)
-        for b in range(X_FIRST, B):
-            load_x(b)
+        load_x(2)
+        load_x(3)
 
         x_grp = {}
         x_codes = {}
         x_scales = {}
 
         def regroup_x(b):
-            t = xg_pool.tile([P, 2, D, 4], BF16, name="x_grp", align_bytes=64)
+            t = xg_pool.tile([P, 2 * D, 4], BF16, name="x_grp", align_bytes=64)
             for g in range(2):
-                copy(X_ENG[b], t[:, g, :, :], x_raw[b][:, 4 * g : 4 * (g + 1), :].rearrange("p t d -> p d t"))
+                copy(
+                    X_ENG[b],
+                    t[:, D * g : D * (g + 1), :],
+                    x_raw[b][:, 4 * g : 4 * (g + 1), :].rearrange("p t d -> p d t"),
+                )
             x_grp[b] = t
 
         def quant_x(b):
             c = keep.tile([P, 512], U32, name="x_codes%d" % b, align_bytes=64)
             sc = keep.tile([P, 512], U8, name="x_scales%d" % b, align_bytes=64)
-            nc.vector.quantize_mx(
-                out=c[:].bitcast(FP8X4), scales=sc[:], in_=x_grp[b][:].rearrange("p g d t -> p (g d t)")
-            )
+            nc.vector.quantize_mx(out=c[:].bitcast(FP8X4), scales=sc[:], in_=x_grp[b][:].rearrange("p d t -> p (d t)"))
             x_codes[b] = c
             x_scales[b] = sc
 
@@ -127,36 +121,33 @@ def tile_ginconvfft_pa_t_kernel(tc, x, support, eps, out):
         at_codes = {}
         at_scales = {}
 
-        def transpose_a(s, gu, engs):
-            a32 = a_raw[gu // 2][:, 2 * (gu % 2) + s, :].bitcast(F32)
-            grp = atg_pool.tile([P, 2048], BF16, name="at_grp", align_bytes=64)
+        def transpose_a(gu):
+            grp = atg_pool.tile([P, S * 2048], BF16, name="at_grp", align_bytes=64)
             g32 = grp[:].bitcast(F32)
-            banks = []
-            for g in range(2):
-                bank = psum.tile([P, 512], F32, name="bank", tag="bank")
-                for u in range(2):
-                    for e in range(2):
-                        w0 = 512 * e + 256 * g + 128 * u
-                        nc.tensor.transpose(
-                            out=bank[:, 256 * u + 128 * e : 256 * u + 128 * (e + 1)],
-                            in_=a32[:, w0 : w0 + 128],
-                            identity=ident[:],
-                        )
-                banks.append(bank)
-            for g in range(2):
-                copy(
-                    engs[g],
-                    g32[:, 512 * g : 512 * (g + 1)].rearrange("p (w u) -> p w u", u=2),
-                    banks[g][:].rearrange("p (u w) -> p w u", u=2),
-                )
-            at_grp[(s, gu)] = grp
+            for s in range(S):
+                a32 = a_raw[gu // 2][:, 2 * (gu % 2) + s, :].bitcast(F32)
+                for g in range(2):
+                    bank = psum.tile([P, 512], F32, name="bank", tag="bank")
+                    for u in range(2):
+                        for e in range(2):
+                            w0 = 512 * e + 256 * g + 128 * u
+                            nc.tensor.transpose(
+                                out=bank[:, 256 * u + 128 * e : 256 * u + 128 * (e + 1)],
+                                in_=a32[:, w0 : w0 + 128],
+                                identity=ident[:],
+                            )
+                    nc.scalar.copy(
+                        out=g32[:, 1024 * s + 512 * g : 1024 * s + 512 * (g + 1)].rearrange("p (w u) -> p w u", u=2),
+                        in_=bank[:].rearrange("p (u w) -> p w u", u=2),
+                    )
+            at_grp[gu] = grp
 
-        def quant_a(s, gu):
-            c = keep.tile([P, 512], U32, name="at_codes%d_%d" % (s, gu), align_bytes=64)
-            sc = keep.tile([P, 512], U8, name="at_scales%d_%d" % (s, gu), align_bytes=64)
-            nc.vector.quantize_mx(out=c[:].bitcast(FP8X4), scales=sc[:], in_=at_grp[(s, gu)][:])
-            at_codes[(s, gu)] = c
-            at_scales[(s, gu)] = sc
+        def quant_a(gu):
+            c = keep.tile([P, S * 512], U32, name="at_codes%d" % gu, align_bytes=64)
+            sc = keep.tile([P, S * 512], U8, name="at_scales%d" % gu, align_bytes=64)
+            nc.vector.quantize_mx(out=c[:].bitcast(FP8X4), scales=sc[:], in_=at_grp[gu][:])
+            at_codes[gu] = c
+            at_scales[gu] = sc
 
         state = {"later": []}
 
@@ -176,23 +167,29 @@ def tile_ginconvfft_pa_t_kernel(tc, x, support, eps, out):
         h_codes = {}
         h_scales = {}
 
-        def mx_bank(nt, rhs_of):
-            gu, e = nt // 2, nt % 2
-            bank = psum.tile([P, 512], F32, name="bank", tag="bank")
+        def mx_unit(gu, rhs_of):
+            banks = [psum.tile([P, 512], F32, name="bank", tag="bank") for e in range(2)]
             for s in range(S):
                 for g in range(2):
-                    cols = slice(256 * g + 128 * e, 256 * g + 128 * (e + 1))
-                    rc, rs = rhs_of(s, g)
-                    nc.tensor.matmul_mx(
-                        out=bank[:, D * s : D * (s + 1)],
-                        lhsT=at_codes[(s, gu)][:, cols].bitcast(FP8X4),
-                        lhsT_scale=at_scales[(s, gu)][:, cols],
-                        rhs=rc.bitcast(FP8X4),
-                        rhs_scale=rs,
-                        start=(g == 0),
-                        stop=(g == 1),
-                    )
-            return bank
+                    for e in range(2):
+                        c0 = 512 * s + 256 * g + 128 * e
+                        rc, rs = rhs_of(s, g)
+                        nc.tensor.matmul_mx(
+                            out=banks[e][:, D * s : D * (s + 1)],
+                            lhsT=at_codes[gu][:, c0 : c0 + 128].bitcast(FP8X4),
+                            lhsT_scale=at_scales[gu][:, c0 : c0 + 128],
+                            rhs=rc.bitcast(FP8X4),
+                            rhs_scale=rs,
+                            start=(g == 0),
+                            stop=(g == 1),
+                        )
+            return banks
+
+        def regroup_h(b, g, engs):
+            grp = hg_pool.tile([P, S, D, 4], BF16, name="h_grp", align_bytes=64)
+            for s in range(S):
+                copy(engs[s], grp[:, s, :, :], hh[(b, g)][:, :, 0, :, s].rearrange("p t c -> p c t"))
+            return grp
 
         def quant_h(b, g, grp):
             c = hc_pool.tile([P, 512], U32, name="h_codes", align_bytes=64)
@@ -201,50 +198,36 @@ def tile_ginconvfft_pa_t_kernel(tc, x, support, eps, out):
             h_codes[(b, g)] = c
             h_scales[(b, g)] = sc
 
-        def hop1_mm(b, nt):
-            return mx_bank(nt, lambda s, gk: (x_codes[b][:, D * gk : D * (gk + 1)], x_scales[b][:, D * gk : D * (gk + 1)]))
+        def hop1_mm(b, gu):
+            return mx_unit(gu, lambda s, gk: (x_codes[b][:, D * gk : D * (gk + 1)], x_scales[b][:, D * gk : D * (gk + 1)]))
 
-        def hop1_add(b, nt, bank):
-            g, t = nt // 4, nt % 4
-            if t == 0:
+        def hop1_add(b, gu, banks):
+            g = gu // 2
+            if gu % 2 == 0:
                 hh[(b, g)] = hh_pool.tile([P, 4, 2, D, S], F32, name="hh", tag="hh")
-            tl = hh[(b, g)]
-            nc.vector.scalar_tensor_tensor(
-                out=tl[:, t, 0, :, :],
-                in0=x_raw[b][:, nt, :].unsqueeze(2).to_broadcast([P, D, S]),
-                scalar=gain[:, 0:1],
-                in1=bank[:].rearrange("p (s c) -> p c s", s=S),
-                op0=MULT,
-                op1=ADD,
-            )
-            tick()
-            if t == 3 and b > 0:
-                grp = regroup_h(b, g, R_ENG[2 * b + g])
-                defer(DEFER_H, lambda: quant_h(b, g, grp))
-
-        def regroup_h(b, g, engs):
-            grp = hg_pool.tile([P, S, D, 4], BF16, name="h_grp", align_bytes=64)
-            for s in range(S):
-                copy(engs[s], grp[:, s, :, :], hh[(b, g)][:, :, 0, :, s].rearrange("p t c -> p c t"))
-            return grp
+            for e in range(2):
+                nt = 2 * gu + e
+                nc.vector.scalar_tensor_tensor(
+                    out=hh[(b, g)][:, nt % 4, 0, :, :],
+                    in0=x_raw[b][:, nt, :].unsqueeze(2).to_broadcast([P, D, S]),
+                    scalar=gain[:, 0:1],
+                    in1=banks[e][:].rearrange("p (s c) -> p c s", s=S),
+                    op0=MULT,
+                    op1=ADD,
+                )
+                tick()
 
         def hop1_unit(b, gu):
-            banks = [hop1_mm(b, 2 * gu + e) for e in range(2)]
-            for e in range(2):
-                hop1_add(b, 2 * gu + e, banks[e])
+            hop1_add(b, gu, hop1_mm(b, gu))
+            if gu % 2 == 1:
+                grp = regroup_h(b, gu // 2, R_ENG)
+                defer(DEFER_H, lambda: quant_h(b, gu // 2, grp))
 
-        def hop2_unit(b, gu, ilv, split):
-            banks = []
-            for e in range(2):
-                banks.append(
-                    mx_bank(
-                        2 * gu + e,
-                        lambda s, gk: (
-                            h_codes[(b, gk)][:, D * s : D * (s + 1)],
-                            h_scales[(b, gk)][:, D * s : D * (s + 1)],
-                        ),
-                    )
-                )
+        def hop2_unit(b, gu, engs):
+            banks = mx_unit(
+                gu,
+                lambda s, gk: (h_codes[(b, gk)][:, D * s : D * (s + 1)], h_scales[(b, gk)][:, D * s : D * (s + 1)]),
+            )
             o = o_pool.tile([P, 2, 4 * D], F32, name="o")
             tl = hh[(b, gu // 2)]
             for e in range(2):
@@ -261,82 +244,49 @@ def tile_ginconvfft_pa_t_kernel(tc, x, support, eps, out):
             for e in range(2):
                 t = (2 * gu + e) % 4
                 copy(
-                    ilv[e],
+                    engs[e],
                     o[:, e, :].rearrange("p (f j) -> p f j", j=2),
                     tl[:, t, :, :, :].rearrange("p j c s -> p (c s) j"),
                 )
-                if split:
-                    nc.sync.dma_start(
-                        out=out[b, 256 * gu : 256 * (gu + 1)].rearrange("(p e) l f -> p e (l f)", e=2)[:, e, :],
-                        in_=o[:, e, :],
-                    )
-            if not split:
-                nc.sync.dma_start(
-                    out=out[b, 256 * gu : 256 * (gu + 1)].rearrange("(p e) l f -> p (e l f)", e=2),
-                    in_=o[:].rearrange("p e f -> p (e f)"),
-                )
+            nc.sync.dma_start(
+                out=out[b, 256 * gu : 256 * (gu + 1)].rearrange("(p e) l f -> p (e l f)", e=2),
+                in_=o[:].rearrange("p e f -> p (e f)"),
+            )
 
-        for b in range(X_FIRST):
-            regroup_x(b)
-            quant_x(b)
-        bank_of = {}
+        regroup_x(0)
+        regroup_x(1)
+        quant_x(0)
+        quant_x(1)
+        transpose_a(0)
+        quant_a(0)
+        grps = {}
+        for gu in range(4):
+            if gu + 1 < 4:
+                transpose_a(gu + 1)
+            banks0 = hop1_mm(0, gu)
+            banks1 = hop1_mm(1, gu)
+            hop1_add(0, gu, banks0)
+            if gu + 1 < 4:
+                quant_a(gu + 1)
+            hop1_add(1, gu, banks1)
+            if gu == 3:
+                for g in range(2):
+                    grps[(0, g)] = regroup_h(0, g, R_START[(0, g)])
+                for g in range(2):
+                    grps[(1, g)] = regroup_h(1, g, R_START[(1, g)])
+        for g in range(2):
+            quant_h(0, g, grps[(0, g)])
+        regroup_x(2)
+        regroup_x(3)
+        defer(2, lambda: quant_h(1, 0, grps[(1, 0)]))
+        defer(4, lambda: quant_h(1, 1, grps[(1, 1)]))
 
-        def mm(nts):
-            for nt in nts:
-                bank_of[nt] = hop1_mm(0, nt)
-
-        def add(nts):
-            for nt in nts:
-                hop1_add(0, nt, bank_of[nt])
-
-        for gu in range(2):
-            for s in range(S):
-                transpose_a(s, gu, E_ENG[2 * gu + s])
-                quant_a(s, gu)
-        mm([0, 1])
-        transpose_a(0, 2, E_ENG[4])
-        transpose_a(1, 2, E_ENG[5])
-        add([0, 1])
-        quant_a(0, 2)
-        quant_a(1, 2)
-        mm([2])
-        transpose_a(0, 3, E_ENG[6])
-        transpose_a(1, 3, E_ENG[7])
-        if X_FIRST < 2:
-            regroup_x(1)
-        add([2])
-        mm([3, 4, 5])
-        add([3])
-        grp00 = regroup_h(0, 0, R_ENG[0])
-        quant_a(0, 3)
-        add([4])
-        quant_a(1, 3)
-        add([5])
-        mm([6, 7])
-        add([6, 7])
-        grp01 = regroup_h(0, 1, R_ENG[1])
-        quant_h(0, 0, grp00)
-        if X_FIRST < 2:
-            quant_x(1)
-        quant_h(0, 1, grp01)
-        if X_FIRST < 3 and XR2_AT < 0:
-            regroup_x(2)
-
-        ones = [(b, gu) for b in range(1, B) for gu in range(4)]
+        ones = [(b, gu) for b in range(2, B) for gu in range(4)]
         twos = [(b, gu) for b in range(B) for gu in range(4)]
-        for b, gu in ones[:PRE]:
-            hop1_unit(b, gu)
-        ones = ones[PRE:]
         for i, (b, gu) in enumerate(twos):
-            hop2_unit(b, gu, ILV[i], i >= len(twos) - SPLIT_STORES)
-            if i == XR2_AT and X_FIRST < 3:
-                regroup_x(2)
-            if i == XR3_AT and X_FIRST < 4:
-                regroup_x(3)
-            if i == XQ2_AT and X_FIRST < 3:
-                quant_x(2)
-            if i == XQ3_AT and X_FIRST < 4:
-                quant_x(3)
+            hop2_unit(b, gu, ILV[i])
+            if i in XQ_AT:
+                quant_x(XQ_AT[i])
             for b1, gu1 in ones[: RATES[i]]:
                 hop1_unit(b1, gu1)
             ones = ones[RATES[i] :]

@@ -19,24 +19,33 @@ NT = 8
 FLOPS = 4 * 2 * 1024 * 1024 * 1024
 
 MANUAL = False
-DEFER_H = 4
-X_ENG = ["g", "s", "g", "g"]
-R_START = {(0, 0): "ss", (1, 0): "sg", (0, 1): "ss", (1, 1): "sg"}
-R_ENG = "ss"
-RATES = [1, 1, 1, 0, 1, 1, 1, 1, 1, 0, 0, 0, 0, 0, 0, 0]
-ILV = ["sg", "sg", "sg", "sg", "sg", "sg", "sg", "sg", "sg", "sg", "sg", "sg", "sg", "sg", "sg", "sv"]
+DEFER_H = 2
+PRE = 1
+X_ENG = ["v", "s", "s", "s"]
+R_ENG = ["ss", "sg", "gs", "sg", "gs", "gg", "gs", "vs"]
+ILV = ["sg", "gs", "sg", "sg", "sv", "gs", "ss", "ss", "sg", "sg", "ss", "sv", "sv", "gs", "sv", "sg"]
+E_ENG = ["vv", "ss", "vs", "ss", "sv", "ss", "ss", "sv"]
 G_SPLIT = 2
+EPS_MM = True
+X_FIRST = 1
+XG_BUFS = 2
+SPLIT_STORES = 0
+E_LAST = ["s", "s"]
+XR2_AT = 0
+XR3_AT = 4
+XQ2_AT = 0
+XQ3_AT = 4
+RATES = [1, 1, 1, 3, 0, 1, 0, 0, 0, 1, 3, 0, 0, 1, 0, 0]
 HH_BUFS = 6
 O_BUFS = 4
-XQ_AT = {0: 2, 3: 3}
 
 
 def tile_ginconvfft_pa_t_kernel(tc, x, support, eps, out):
     nc = tc.nc
     with ExitStack() as ctx:
         keep = ctx.enter_context(tc.tile_pool(name="keep", bufs=1))
-        atg_pool = ctx.enter_context(tc.tile_pool(name="atg", bufs=2))
-        xg_pool = ctx.enter_context(tc.tile_pool(name="xg", bufs=2))
+        atg_pool = ctx.enter_context(tc.tile_pool(name="atg", bufs=4))
+        xg_pool = ctx.enter_context(tc.tile_pool(name="xg", bufs=XG_BUFS))
         hh_pool = ctx.enter_context(tc.tile_pool(name="hh", bufs=HH_BUFS))
         hg_pool = ctx.enter_context(tc.tile_pool(name="hg", bufs=3))
         hc_pool = ctx.enter_context(tc.tile_pool(name="hc", bufs=6))
@@ -64,10 +73,20 @@ def tile_ginconvfft_pa_t_kernel(tc, x, support, eps, out):
 
         ident = keep.tile([P, P], F32, name="ident")
         make_identity(nc, ident[:])
-        eps_sb = keep.tile([P, 1], BF16, name="eps_sb")
-        nc.scalar.dma_start(out=eps_sb[:], in_=eps.partition_broadcast(P))
         gain = keep.tile([P, 1], F32, name="gain")
-        nc.vector.tensor_scalar_add(out=gain[:], in0=eps_sb[:], scalar1=1.0)
+        if EPS_MM:
+            eps_row = keep.tile([P, 32], BF16, name="eps_row")
+            nc.vector.memset(eps_row[:], 0.0)
+            ones = keep.tile([P, P], BF16, name="ones")
+            nc.vector.memset(ones[:], 1.0)
+            nc.scalar.dma_start(out=eps_row[0:1, 0:1], in_=eps.rearrange("(o n) -> o n", o=1))
+            eps_bank = psum.tile([P, 512], F32, name="bank", tag="bank")
+            nc.tensor.matmul(out=eps_bank[:, 0:32], lhsT=ones[:], rhs=eps_row[:], start=True, stop=True)
+            nc.vector.tensor_scalar_add(out=gain[:], in0=eps_bank[:, 0:1], scalar1=1.0)
+        else:
+            eps_sb = keep.tile([P, 1], BF16, name="eps_sb")
+            nc.scalar.dma_start(out=eps_sb[:], in_=eps.partition_broadcast(P))
+            nc.vector.tensor_scalar_add(out=gain[:], in0=eps_sb[:], scalar1=1.0)
 
         x_raw = {}
         a_raw = {}
@@ -88,32 +107,30 @@ def tile_ginconvfft_pa_t_kernel(tc, x, support, eps, out):
                 in_=support[s, 256 * gu : 256 * (gu + 1), :].rearrange("(p e) m -> p (e m)", e=2),
             )
 
-        load_x(0)
-        load_x(1)
+        for b in range(X_FIRST):
+            load_x(b)
         for gu in range(4):
             for s in range(S):
                 load_a(s, gu)
-        load_x(2)
-        load_x(3)
+        for b in range(X_FIRST, B):
+            load_x(b)
 
         x_grp = {}
         x_codes = {}
         x_scales = {}
 
         def regroup_x(b):
-            t = xg_pool.tile([P, 2 * D, 4], BF16, name="x_grp", align_bytes=64)
+            t = xg_pool.tile([P, 2, D, 4], BF16, name="x_grp", align_bytes=64)
             for g in range(2):
-                copy(
-                    X_ENG[b],
-                    t[:, D * g : D * (g + 1), :],
-                    x_raw[b][:, 4 * g : 4 * (g + 1), :].rearrange("p t d -> p d t"),
-                )
+                copy(X_ENG[b], t[:, g, :, :], x_raw[b][:, 4 * g : 4 * (g + 1), :].rearrange("p t d -> p d t"))
             x_grp[b] = t
 
         def quant_x(b):
             c = keep.tile([P, 512], U32, name="x_codes%d" % b, align_bytes=64)
             sc = keep.tile([P, 512], U8, name="x_scales%d" % b, align_bytes=64)
-            nc.vector.quantize_mx(out=c[:].bitcast(FP8X4), scales=sc[:], in_=x_grp[b][:].rearrange("p d t -> p (d t)"))
+            nc.vector.quantize_mx(
+                out=c[:].bitcast(FP8X4), scales=sc[:], in_=x_grp[b][:].rearrange("p g d t -> p (g d t)")
+            )
             x_codes[b] = c
             x_scales[b] = sc
 
@@ -121,33 +138,36 @@ def tile_ginconvfft_pa_t_kernel(tc, x, support, eps, out):
         at_codes = {}
         at_scales = {}
 
-        def transpose_a(gu):
-            grp = atg_pool.tile([P, S * 2048], BF16, name="at_grp", align_bytes=64)
+        def transpose_a(s, gu, engs):
+            a32 = a_raw[gu // 2][:, 2 * (gu % 2) + s, :].bitcast(F32)
+            grp = atg_pool.tile([P, 2048], BF16, name="at_grp", align_bytes=64)
             g32 = grp[:].bitcast(F32)
-            for s in range(S):
-                a32 = a_raw[gu // 2][:, 2 * (gu % 2) + s, :].bitcast(F32)
-                for g in range(2):
-                    bank = psum.tile([P, 512], F32, name="bank", tag="bank")
-                    for u in range(2):
-                        for e in range(2):
-                            w0 = 512 * e + 256 * g + 128 * u
-                            nc.tensor.transpose(
-                                out=bank[:, 256 * u + 128 * e : 256 * u + 128 * (e + 1)],
-                                in_=a32[:, w0 : w0 + 128],
-                                identity=ident[:],
-                            )
-                    nc.scalar.copy(
-                        out=g32[:, 1024 * s + 512 * g : 1024 * s + 512 * (g + 1)].rearrange("p (w u) -> p w u", u=2),
-                        in_=bank[:].rearrange("p (u w) -> p w u", u=2),
-                    )
-            at_grp[gu] = grp
+            banks = []
+            for g in range(2):
+                bank = psum.tile([P, 512], F32, name="bank", tag="bank")
+                for u in range(2):
+                    for e in range(2):
+                        w0 = 512 * e + 256 * g + 128 * u
+                        nc.tensor.transpose(
+                            out=bank[:, 256 * u + 128 * e : 256 * u + 128 * (e + 1)],
+                            in_=a32[:, w0 : w0 + 128],
+                            identity=ident[:],
+                        )
+                banks.append(bank)
+            for g in range(2):
+                copy(
+                    engs[g],
+                    g32[:, 512 * g : 512 * (g + 1)].rearrange("p (w u) -> p w u", u=2),
+                    banks[g][:].rearrange("p (u w) -> p w u", u=2),
+                )
+            at_grp[(s, gu)] = grp
 
-        def quant_a(gu):
-            c = keep.tile([P, S * 512], U32, name="at_codes%d" % gu, align_bytes=64)
-            sc = keep.tile([P, S * 512], U8, name="at_scales%d" % gu, align_bytes=64)
-            nc.vector.quantize_mx(out=c[:].bitcast(FP8X4), scales=sc[:], in_=at_grp[gu][:])
-            at_codes[gu] = c
-            at_scales[gu] = sc
+        def quant_a(s, gu):
+            c = keep.tile([P, 512], U32, name="at_codes%d_%d" % (s, gu), align_bytes=64)
+            sc = keep.tile([P, 512], U8, name="at_scales%d_%d" % (s, gu), align_bytes=64)
+            nc.vector.quantize_mx(out=c[:].bitcast(FP8X4), scales=sc[:], in_=at_grp[(s, gu)][:])
+            at_codes[(s, gu)] = c
+            at_scales[(s, gu)] = sc
 
         state = {"later": []}
 
@@ -167,29 +187,23 @@ def tile_ginconvfft_pa_t_kernel(tc, x, support, eps, out):
         h_codes = {}
         h_scales = {}
 
-        def mx_unit(gu, rhs_of):
-            banks = [psum.tile([P, 512], F32, name="bank", tag="bank") for e in range(2)]
+        def mx_bank(nt, rhs_of):
+            gu, e = nt // 2, nt % 2
+            bank = psum.tile([P, 512], F32, name="bank", tag="bank")
             for s in range(S):
                 for g in range(2):
-                    for e in range(2):
-                        c0 = 512 * s + 256 * g + 128 * e
-                        rc, rs = rhs_of(s, g)
-                        nc.tensor.matmul_mx(
-                            out=banks[e][:, D * s : D * (s + 1)],
-                            lhsT=at_codes[gu][:, c0 : c0 + 128].bitcast(FP8X4),
-                            lhsT_scale=at_scales[gu][:, c0 : c0 + 128],
-                            rhs=rc.bitcast(FP8X4),
-                            rhs_scale=rs,
-                            start=(g == 0),
-                            stop=(g == 1),
-                        )
-            return banks
-
-        def regroup_h(b, g, engs):
-            grp = hg_pool.tile([P, S, D, 4], BF16, name="h_grp", align_bytes=64)
-            for s in range(S):
-                copy(engs[s], grp[:, s, :, :], hh[(b, g)][:, :, 0, :, s].rearrange("p t c -> p c t"))
-            return grp
+                    cols = slice(256 * g + 128 * e, 256 * g + 128 * (e + 1))
+                    rc, rs = rhs_of(s, g)
+                    nc.tensor.matmul_mx(
+                        out=bank[:, D * s : D * (s + 1)],
+                        lhsT=at_codes[(s, gu)][:, cols].bitcast(FP8X4),
+                        lhsT_scale=at_scales[(s, gu)][:, cols],
+                        rhs=rc.bitcast(FP8X4),
+                        rhs_scale=rs,
+                        start=(g == 0),
+                        stop=(g == 1),
+                    )
+            return bank
 
         def quant_h(b, g, grp):
             c = hc_pool.tile([P, 512], U32, name="h_codes", align_bytes=64)
@@ -198,36 +212,50 @@ def tile_ginconvfft_pa_t_kernel(tc, x, support, eps, out):
             h_codes[(b, g)] = c
             h_scales[(b, g)] = sc
 
-        def hop1_mm(b, gu):
-            return mx_unit(gu, lambda s, gk: (x_codes[b][:, D * gk : D * (gk + 1)], x_scales[b][:, D * gk : D * (gk + 1)]))
+        def hop1_mm(b, nt):
+            return mx_bank(nt, lambda s, gk: (x_codes[b][:, D * gk : D * (gk + 1)], x_scales[b][:, D * gk : D * (gk + 1)]))
 
-        def hop1_add(b, gu, banks):
-            g = gu // 2
-            if gu % 2 == 0:
+        def hop1_add(b, nt, bank):
+            g, t = nt // 4, nt % 4
+            if t == 0:
                 hh[(b, g)] = hh_pool.tile([P, 4, 2, D, S], F32, name="hh", tag="hh")
-            for e in range(2):
-                nt = 2 * gu + e
-                nc.vector.scalar_tensor_tensor(
-                    out=hh[(b, g)][:, nt % 4, 0, :, :],
-                    in0=x_raw[b][:, nt, :].unsqueeze(2).to_broadcast([P, D, S]),
-                    scalar=gain[:, 0:1],
-                    in1=banks[e][:].rearrange("p (s c) -> p c s", s=S),
-                    op0=MULT,
-                    op1=ADD,
-                )
-                tick()
+            tl = hh[(b, g)]
+            nc.vector.scalar_tensor_tensor(
+                out=tl[:, t, 0, :, :],
+                in0=x_raw[b][:, nt, :].unsqueeze(2).to_broadcast([P, D, S]),
+                scalar=gain[:, 0:1],
+                in1=bank[:].rearrange("p (s c) -> p c s", s=S),
+                op0=MULT,
+                op1=ADD,
+            )
+            tick()
+            if t == 3 and b > 0:
+                grp = regroup_h(b, g, R_ENG[2 * b + g])
+                defer(DEFER_H, lambda: quant_h(b, g, grp))
+
+        def regroup_h(b, g, engs):
+            grp = hg_pool.tile([P, S, D, 4], BF16, name="h_grp", align_bytes=64)
+            for s in range(S):
+                copy(engs[s], grp[:, s, :, :], hh[(b, g)][:, :, 0, :, s].rearrange("p t c -> p c t"))
+            return grp
 
         def hop1_unit(b, gu):
-            hop1_add(b, gu, hop1_mm(b, gu))
-            if gu % 2 == 1:
-                grp = regroup_h(b, gu // 2, R_ENG)
-                defer(DEFER_H, lambda: quant_h(b, gu // 2, grp))
+            banks = [hop1_mm(b, 2 * gu + e) for e in range(2)]
+            for e in range(2):
+                hop1_add(b, 2 * gu + e, banks[e])
 
-        def hop2_unit(b, gu, engs):
-            banks = mx_unit(
-                gu,
-                lambda s, gk: (h_codes[(b, gk)][:, D * s : D * (s + 1)], h_scales[(b, gk)][:, D * s : D * (s + 1)]),
-            )
+        def hop2_unit(b, gu, ilv, split):
+            banks = []
+            for e in range(2):
+                banks.append(
+                    mx_bank(
+                        2 * gu + e,
+                        lambda s, gk: (
+                            h_codes[(b, gk)][:, D * s : D * (s + 1)],
+                            h_scales[(b, gk)][:, D * s : D * (s + 1)],
+                        ),
+                    )
+                )
             o = o_pool.tile([P, 2, 4 * D], F32, name="o")
             tl = hh[(b, gu // 2)]
             for e in range(2):
@@ -244,49 +272,82 @@ def tile_ginconvfft_pa_t_kernel(tc, x, support, eps, out):
             for e in range(2):
                 t = (2 * gu + e) % 4
                 copy(
-                    engs[e],
+                    ilv[e],
                     o[:, e, :].rearrange("p (f j) -> p f j", j=2),
                     tl[:, t, :, :, :].rearrange("p j c s -> p (c s) j"),
                 )
-            nc.sync.dma_start(
-                out=out[b, 256 * gu : 256 * (gu + 1)].rearrange("(p e) l f -> p (e l f)", e=2),
-                in_=o[:].rearrange("p e f -> p (e f)"),
-            )
+                if split:
+                    nc.sync.dma_start(
+                        out=out[b, 256 * gu : 256 * (gu + 1)].rearrange("(p e) l f -> p e (l f)", e=2)[:, e, :],
+                        in_=o[:, e, :],
+                    )
+            if not split:
+                nc.sync.dma_start(
+                    out=out[b, 256 * gu : 256 * (gu + 1)].rearrange("(p e) l f -> p (e l f)", e=2),
+                    in_=o[:].rearrange("p e f -> p (e f)"),
+                )
 
-        regroup_x(0)
-        regroup_x(1)
-        quant_x(0)
-        quant_x(1)
-        transpose_a(0)
-        quant_a(0)
-        grps = {}
-        for gu in range(4):
-            if gu + 1 < 4:
-                transpose_a(gu + 1)
-            banks0 = hop1_mm(0, gu)
-            banks1 = hop1_mm(1, gu)
-            hop1_add(0, gu, banks0)
-            if gu + 1 < 4:
-                quant_a(gu + 1)
-            hop1_add(1, gu, banks1)
-            if gu == 3:
-                for g in range(2):
-                    grps[(0, g)] = regroup_h(0, g, R_START[(0, g)])
-                for g in range(2):
-                    grps[(1, g)] = regroup_h(1, g, R_START[(1, g)])
-        for g in range(2):
-            quant_h(0, g, grps[(0, g)])
-        regroup_x(2)
-        regroup_x(3)
-        defer(2, lambda: quant_h(1, 0, grps[(1, 0)]))
-        defer(4, lambda: quant_h(1, 1, grps[(1, 1)]))
+        for b in range(X_FIRST):
+            regroup_x(b)
+            quant_x(b)
+        bank_of = {}
 
-        ones = [(b, gu) for b in range(2, B) for gu in range(4)]
+        def mm(nts):
+            for nt in nts:
+                bank_of[nt] = hop1_mm(0, nt)
+
+        def add(nts):
+            for nt in nts:
+                hop1_add(0, nt, bank_of[nt])
+
+        for gu in range(2):
+            for s in range(S):
+                transpose_a(s, gu, E_ENG[2 * gu + s])
+                quant_a(s, gu)
+        mm([0, 1])
+        transpose_a(0, 2, E_ENG[4])
+        transpose_a(1, 2, E_ENG[5])
+        add([0, 1])
+        quant_a(0, 2)
+        quant_a(1, 2)
+        mm([2])
+        transpose_a(0, 3, E_ENG[6])
+        transpose_a(1, 3, E_ENG[7])
+        if X_FIRST < 2:
+            regroup_x(1)
+        add([2])
+        mm([3, 4, 5])
+        add([3])
+        grp00 = regroup_h(0, 0, R_ENG[0])
+        quant_a(0, 3)
+        add([4])
+        quant_a(1, 3)
+        add([5])
+        mm([6, 7])
+        add([6, 7])
+        grp01 = regroup_h(0, 1, R_ENG[1])
+        quant_h(0, 0, grp00)
+        if X_FIRST < 2:
+            quant_x(1)
+        quant_h(0, 1, grp01)
+        if X_FIRST < 3 and XR2_AT < 0:
+            regroup_x(2)
+
+        ones = [(b, gu) for b in range(1, B) for gu in range(4)]
         twos = [(b, gu) for b in range(B) for gu in range(4)]
+        for b, gu in ones[:PRE]:
+            hop1_unit(b, gu)
+        ones = ones[PRE:]
         for i, (b, gu) in enumerate(twos):
-            hop2_unit(b, gu, ILV[i])
-            if i in XQ_AT:
-                quant_x(XQ_AT[i])
+            hop2_unit(b, gu, ILV[i], i >= len(twos) - SPLIT_STORES)
+            if i == XR2_AT and X_FIRST < 3:
+                regroup_x(2)
+            if i == XR3_AT and X_FIRST < 4:
+                regroup_x(3)
+            if i == XQ2_AT and X_FIRST < 3:
+                quant_x(2)
+            if i == XQ3_AT and X_FIRST < 4:
+                quant_x(3)
             for b1, gu1 in ones[: RATES[i]]:
                 hop1_unit(b1, gu1)
             ones = ones[RATES[i] :]

@@ -15,339 +15,210 @@ P = 128
 B = 4
 D = 256
 S = 2
-NT = 8
+QUARTERS = 4
 FLOPS = 4 * 2 * 1024 * 1024 * 1024
 
-MANUAL = False
-DEFER_H = 2
-PRE = 1
-X_ENG = ["v", "s", "s", "s"]
-R_ENG = ["ss", "sg", "gs", "sg", "gs", "gg", "gs", "vs"]
-ILV = ["sg", "gs", "sg", "sg", "sv", "gs", "ss", "ss", "sg", "sg", "ss", "sv", "sv", "gs", "sv", "sg"]
-E_ENG = ["vv", "ss", "vs", "ss", "sv", "ss", "ss", "sv"]
-G_SPLIT = 2
-EPS_MM = True
-X_FIRST = 1
-XG_BUFS = 2
-SPLIT_STORES = 0
-E_LAST = ["s", "s"]
-XR2_AT = 0
-XR3_AT = 4
-XQ2_AT = 0
-XQ3_AT = 4
-RATES = [1, 1, 1, 3, 0, 1, 0, 0, 0, 1, 3, 0, 0, 1, 0, 0]
-HH_BUFS = 6
-O_BUFS = 4
+LEAD = 1
 
 
 def tile_ginconvfft_pa_t_kernel(tc, x, support, eps, out):
     nc = tc.nc
     with ExitStack() as ctx:
         keep = ctx.enter_context(tc.tile_pool(name="keep", bufs=1))
-        atg_pool = ctx.enter_context(tc.tile_pool(name="atg", bufs=4))
-        xg_pool = ctx.enter_context(tc.tile_pool(name="xg", bufs=XG_BUFS))
-        hh_pool = ctx.enter_context(tc.tile_pool(name="hh", bufs=HH_BUFS))
-        hg_pool = ctx.enter_context(tc.tile_pool(name="hg", bufs=3))
-        hc_pool = ctx.enter_context(tc.tile_pool(name="hc", bufs=6))
-        o_pool = ctx.enter_context(tc.tile_pool(name="o", bufs=O_BUFS))
+        at_stage = ctx.enter_context(tc.tile_pool(name="at_stage", bufs=4))
+        x_stage = ctx.enter_context(tc.tile_pool(name="x_stage", bufs=2))
+        h_stage = ctx.enter_context(tc.tile_pool(name="h_stage", bufs=3))
+        big = ctx.enter_context(tc.tile_pool(name="big", bufs=6))
+        h_mx = ctx.enter_context(tc.tile_pool(name="h_mx", bufs=6))
+        rows = ctx.enter_context(tc.tile_pool(name="rows", bufs=4))
         psum = ctx.enter_context(tc.psum_pool(name="psum", bufs=8))
-        if MANUAL:
-            ctx.enter_context(tc.manual_schedule())
 
-        def copy(eng, dst, src):
-            if eng == "v":
-                nc.vector.tensor_copy(out=dst, in_=src)
-            elif eng == "s":
-                nc.scalar.copy(out=dst, in_=src)
-            else:
-                n = dst.shape[1] // G_SPLIT
-                for i in range(G_SPLIT):
-                    nc.gpsimd.tensor_scalar(
-                        out=dst[:, i * n : (i + 1) * n],
-                        in0=src[:, i * n : (i + 1) * n],
-                        scalar1=1.0,
-                        scalar2=0.0,
-                        op0=MULT,
-                        op1=ADD,
-                    )
+        def vector_copy(dst, src):
+            nc.vector.tensor_copy(out=dst, in_=src)
+
+        def scalar_copy(dst, src):
+            nc.scalar.copy(out=dst, in_=src)
+
+        def gpsimd_copy(dst, src):
+            nc.gpsimd.tensor_scalar(out=dst, in0=src, scalar1=1.0, scalar2=0.0, op0=MULT, op1=ADD)
 
         ident = keep.tile([P, P], F32, name="ident")
         make_identity(nc, ident[:])
-        gain = keep.tile([P, 1], F32, name="gain")
-        if EPS_MM:
-            eps_row = keep.tile([P, 32], BF16, name="eps_row")
-            nc.vector.memset(eps_row[:], 0.0)
-            ones = keep.tile([P, P], BF16, name="ones")
-            nc.vector.memset(ones[:], 1.0)
-            nc.scalar.dma_start(out=eps_row[0:1, 0:1], in_=eps.rearrange("(o n) -> o n", o=1))
-            eps_bank = psum.tile([P, 512], F32, name="bank", tag="bank")
-            nc.tensor.matmul(out=eps_bank[:, 0:32], lhsT=ones[:], rhs=eps_row[:], start=True, stop=True)
-            nc.vector.tensor_scalar_add(out=gain[:], in0=eps_bank[:, 0:1], scalar1=1.0)
-        else:
-            eps_sb = keep.tile([P, 1], BF16, name="eps_sb")
-            nc.scalar.dma_start(out=eps_sb[:], in_=eps.partition_broadcast(P))
-            nc.vector.tensor_scalar_add(out=gain[:], in0=eps_sb[:], scalar1=1.0)
 
-        x_raw = {}
-        a_raw = {}
+        eps_row = keep.tile([P, 32], BF16, name="eps_row")
+        nc.vector.memset(eps_row[:], 0.0)
+        ones = keep.tile([P, P], BF16, name="ones")
+        nc.vector.memset(ones[:], 1.0)
+        nc.scalar.dma_start(out=eps_row[0:1, 0:1], in_=eps.rearrange("(o n) -> o n", o=1))
+        eps_bank = psum.tile([P, 512], F32, name="bank")
+        nc.tensor.matmul(out=eps_bank[:, 0:32], lhsT=ones[:], rhs=eps_row[:], start=True, stop=True)
+        gain = keep.tile([P, 1], F32, name="gain")
+        nc.vector.tensor_scalar_add(out=gain[:], in0=eps_bank[:, 0:1], scalar1=1.0)
+
+        x_raw = [keep.tile([P, 2 * QUARTERS, D], BF16, name="x_raw%d" % b) for b in range(B)]
+        a_raw = [big.tile([P, 4, 2048], BF16, name="a_raw", tag="big") for half in range(2)]
 
         def load_x(b):
-            t = keep.tile([P, NT, D], BF16, name="x_raw%d" % b)
             nc.sync.dma_start(
-                out=t[:].rearrange("p (q e) d -> p q (e d)", e=2),
-                in_=x[b].rearrange("(q p e) l h -> p q (e l h)", q=4, p=P, e=2),
-            )
-            x_raw[b] = t
-
-        def load_a(s, gu):
-            if (gu // 2) not in a_raw:
-                a_raw[gu // 2] = hh_pool.tile([P, 4, 2048], BF16, name="a_raw", tag="hh")
-            nc.sync.dma_start(
-                out=a_raw[gu // 2][:, 2 * (gu % 2) + s, :],
-                in_=support[s, 256 * gu : 256 * (gu + 1), :].rearrange("(p e) m -> p (e m)", e=2),
+                out=x_raw[b][:].rearrange("p (q e) d -> p q (e d)", e=2),
+                in_=x[b].rearrange("(q p e) l h -> p q (e l h)", q=QUARTERS, p=P, e=2),
             )
 
-        for b in range(X_FIRST):
-            load_x(b)
-        for gu in range(4):
+        load_x(0)
+        for q in range(QUARTERS):
             for s in range(S):
-                load_a(s, gu)
-        for b in range(X_FIRST, B):
+                nc.sync.dma_start(
+                    out=a_raw[q // 2][:, 2 * (q % 2) + s, :],
+                    in_=support[s, 256 * q : 256 * (q + 1), :].rearrange("(p e) m -> p (e m)", e=2),
+                )
+        for b in range(1, B):
             load_x(b)
 
-        x_grp = {}
         x_codes = {}
         x_scales = {}
 
-        def regroup_x(b):
-            t = xg_pool.tile([P, 2, D, 4], BF16, name="x_grp", align_bytes=64)
+        def quantise_x(b, copy):
+            grouped = x_stage.tile([P, 2, D, 4], BF16, name="x_grouped", align_bytes=64)
             for g in range(2):
-                copy(X_ENG[b], t[:, g, :, :], x_raw[b][:, 4 * g : 4 * (g + 1), :].rearrange("p t d -> p d t"))
-            x_grp[b] = t
-
-        def quant_x(b):
-            c = keep.tile([P, 512], U32, name="x_codes%d" % b, align_bytes=64)
-            sc = keep.tile([P, 512], U8, name="x_scales%d" % b, align_bytes=64)
+                copy(grouped[:, g, :, :], x_raw[b][:, 4 * g : 4 * (g + 1), :].rearrange("p t d -> p d t"))
+            x_codes[b] = keep.tile([P, 2 * D], U32, name="x_codes%d" % b, align_bytes=64)
+            x_scales[b] = keep.tile([P, 2 * D], U8, name="x_scales%d" % b, align_bytes=64)
             nc.vector.quantize_mx(
-                out=c[:].bitcast(FP8X4), scales=sc[:], in_=x_grp[b][:].rearrange("p g d t -> p (g d t)")
+                out=x_codes[b][:].bitcast(FP8X4),
+                scales=x_scales[b][:],
+                in_=grouped[:].rearrange("p g d t -> p (g d t)"),
             )
-            x_codes[b] = c
-            x_scales[b] = sc
 
-        at_grp = {}
         at_codes = {}
         at_scales = {}
 
-        def transpose_a(s, gu, engs):
-            a32 = a_raw[gu // 2][:, 2 * (gu % 2) + s, :].bitcast(F32)
-            grp = atg_pool.tile([P, 2048], BF16, name="at_grp", align_bytes=64)
-            g32 = grp[:].bitcast(F32)
-            banks = []
+        def quantise_a(s, q):
+            words = a_raw[q // 2][:, 2 * (q % 2) + s, :].bitcast(F32)
+            grouped = at_stage.tile([P, 2048], BF16, name="at_grouped", align_bytes=64)
+            grouped_words = grouped[:].bitcast(F32)
             for g in range(2):
-                bank = psum.tile([P, 512], F32, name="bank", tag="bank")
+                bank = psum.tile([P, 512], F32, name="bank")
                 for u in range(2):
                     for e in range(2):
-                        w0 = 512 * e + 256 * g + 128 * u
+                        first_word = 512 * e + 256 * g + 128 * u
                         nc.tensor.transpose(
                             out=bank[:, 256 * u + 128 * e : 256 * u + 128 * (e + 1)],
-                            in_=a32[:, w0 : w0 + 128],
+                            in_=words[:, first_word : first_word + 128],
                             identity=ident[:],
                         )
-                banks.append(bank)
-            for g in range(2):
-                copy(
-                    engs[g],
-                    g32[:, 512 * g : 512 * (g + 1)].rearrange("p (w u) -> p w u", u=2),
-                    banks[g][:].rearrange("p (u w) -> p w u", u=2),
+                scalar_copy(
+                    grouped_words[:, 512 * g : 512 * (g + 1)].rearrange("p (col u) -> p col u", u=2),
+                    bank[:].rearrange("p (u col) -> p col u", u=2),
                 )
-            at_grp[(s, gu)] = grp
+            at_codes[(s, q)] = keep.tile([P, 512], U32, name="at_codes%d_%d" % (s, q), align_bytes=64)
+            at_scales[(s, q)] = keep.tile([P, 512], U8, name="at_scales%d_%d" % (s, q), align_bytes=64)
+            nc.vector.quantize_mx(out=at_codes[(s, q)][:].bitcast(FP8X4), scales=at_scales[(s, q)][:], in_=grouped[:])
 
-        def quant_a(s, gu):
-            c = keep.tile([P, 512], U32, name="at_codes%d_%d" % (s, gu), align_bytes=64)
-            sc = keep.tile([P, 512], U8, name="at_scales%d_%d" % (s, gu), align_bytes=64)
-            nc.vector.quantize_mx(out=c[:].bitcast(FP8X4), scales=sc[:], in_=at_grp[(s, gu)][:])
-            at_codes[(s, gu)] = c
-            at_scales[(s, gu)] = sc
-
-        state = {"later": []}
-
-        def defer(n, fn):
-            state["later"] = state["later"] + [[n, fn]]
-
-        def tick():
-            keep_l = []
-            for n, fn in state["later"]:
-                if n <= 1:
-                    fn()
-                else:
-                    keep_l.append([n - 1, fn])
-            state["later"] = keep_l
-
-        hh = {}
-        h_codes = {}
-        h_scales = {}
-
-        def mx_bank(nt, rhs_of):
-            gu, e = nt // 2, nt % 2
-            bank = psum.tile([P, 512], F32, name="bank", tag="bank")
+        def products(q, e, moving):
+            bank = psum.tile([P, 512], F32, name="bank")
             for s in range(S):
                 for g in range(2):
                     cols = slice(256 * g + 128 * e, 256 * g + 128 * (e + 1))
-                    rc, rs = rhs_of(s, g)
+                    codes, scales = moving(s, g)
                     nc.tensor.matmul_mx(
                         out=bank[:, D * s : D * (s + 1)],
-                        lhsT=at_codes[(s, gu)][:, cols].bitcast(FP8X4),
-                        lhsT_scale=at_scales[(s, gu)][:, cols],
-                        rhs=rc.bitcast(FP8X4),
-                        rhs_scale=rs,
+                        lhsT=at_codes[(s, q)][:, cols].bitcast(FP8X4),
+                        lhsT_scale=at_scales[(s, q)][:, cols],
+                        rhs=codes.bitcast(FP8X4),
+                        rhs_scale=scales,
                         start=(g == 0),
                         stop=(g == 1),
                     )
             return bank
 
-        def quant_h(b, g, grp):
-            c = hc_pool.tile([P, 512], U32, name="h_codes", align_bytes=64)
-            sc = hc_pool.tile([P, 512], U8, name="h_scales", align_bytes=64)
-            nc.vector.quantize_mx(out=c[:].bitcast(FP8X4), scales=sc[:], in_=grp[:].rearrange("p s c t -> p (s c t)"))
-            h_codes[(b, g)] = c
-            h_scales[(b, g)] = sc
-
-        def hop1_mm(b, nt):
-            return mx_bank(nt, lambda s, gk: (x_codes[b][:, D * gk : D * (gk + 1)], x_scales[b][:, D * gk : D * (gk + 1)]))
-
-        def hop1_add(b, nt, bank):
-            g, t = nt // 4, nt % 4
-            if t == 0:
-                hh[(b, g)] = hh_pool.tile([P, 4, 2, D, S], F32, name="hh", tag="hh")
-            tl = hh[(b, g)]
+        def add_self_term(dst, previous, bank):
             nc.vector.scalar_tensor_tensor(
-                out=tl[:, t, 0, :, :],
-                in0=x_raw[b][:, nt, :].unsqueeze(2).to_broadcast([P, D, S]),
+                out=dst,
+                in0=previous,
                 scalar=gain[:, 0:1],
-                in1=bank[:].rearrange("p (s c) -> p c s", s=S),
+                in1=bank[:].rearrange("p (s d) -> p d s", s=S),
                 op0=MULT,
                 op1=ADD,
             )
-            tick()
-            if t == 3 and b > 0:
-                grp = regroup_h(b, g, R_ENG[2 * b + g])
-                defer(DEFER_H, lambda: quant_h(b, g, grp))
 
-        def regroup_h(b, g, engs):
-            grp = hg_pool.tile([P, S, D, 4], BF16, name="h_grp", align_bytes=64)
-            for s in range(S):
-                copy(engs[s], grp[:, s, :, :], hh[(b, g)][:, :, 0, :, s].rearrange("p t c -> p c t"))
-            return grp
+        h = {}
+        h_codes = {}
+        h_scales = {}
 
-        def hop1_unit(b, gu):
-            banks = [hop1_mm(b, 2 * gu + e) for e in range(2)]
-            for e in range(2):
-                hop1_add(b, 2 * gu + e, banks[e])
-
-        def hop2_unit(b, gu, ilv, split):
-            banks = []
-            for e in range(2):
-                banks.append(
-                    mx_bank(
-                        2 * gu + e,
-                        lambda s, gk: (
-                            h_codes[(b, gk)][:, D * s : D * (s + 1)],
-                            h_scales[(b, gk)][:, D * s : D * (s + 1)],
-                        ),
-                    )
+        def hop1(b, q):
+            if q == 0 and b + 1 < B:
+                quantise_x(b + 1, scalar_copy)
+            g = q // 2
+            banks = [
+                products(
+                    q,
+                    e,
+                    lambda s, pass_g: (
+                        x_codes[b][:, D * pass_g : D * (pass_g + 1)],
+                        x_scales[b][:, D * pass_g : D * (pass_g + 1)],
+                    ),
                 )
-            o = o_pool.tile([P, 2, 4 * D], F32, name="o")
-            tl = hh[(b, gu // 2)]
+                for e in range(2)
+            ]
+            if q % 2 == 0:
+                h[(b, g)] = big.tile([P, 4, 2, D, S], F32, name="h", tag="big")
             for e in range(2):
-                t = (2 * gu + e) % 4
-                nc.vector.scalar_tensor_tensor(
-                    out=tl[:, t, 1, :, :],
-                    in0=tl[:, t, 0, :, :],
-                    scalar=gain[:, 0:1],
-                    in1=banks[e][:].rearrange("p (s c) -> p c s", s=S),
-                    op0=MULT,
-                    op1=ADD,
+                add_self_term(
+                    h[(b, g)][:, 2 * (q % 2) + e, 0, :, :],
+                    x_raw[b][:, 2 * q + e, :].unsqueeze(2).to_broadcast([P, D, S]),
+                    banks[e],
                 )
-                tick()
+            if q % 2 == 1:
+                grouped = h_stage.tile([P, S, D, 4], BF16, name="h_grouped", align_bytes=64)
+                for s, copy in enumerate([scalar_copy, gpsimd_copy]):
+                    copy(grouped[:, s, :, :], h[(b, g)][:, :, 0, :, s].rearrange("p t d -> p d t"))
+                h_codes[(b, g)] = h_mx.tile([P, S * D], U32, name="h_codes", align_bytes=64)
+                h_scales[(b, g)] = h_mx.tile([P, S * D], U8, name="h_scales", align_bytes=64)
+                nc.vector.quantize_mx(
+                    out=h_codes[(b, g)][:].bitcast(FP8X4),
+                    scales=h_scales[(b, g)][:],
+                    in_=grouped[:].rearrange("p s d t -> p (s d t)"),
+                )
+
+        def hop2(b, q, second_copy):
+            banks = [
+                products(
+                    q,
+                    e,
+                    lambda s, pass_g: (
+                        h_codes[(b, pass_g)][:, D * s : D * (s + 1)],
+                        h_scales[(b, pass_g)][:, D * s : D * (s + 1)],
+                    ),
+                )
+                for e in range(2)
+            ]
+            both = h[(b, q // 2)]
             for e in range(2):
-                t = (2 * gu + e) % 4
+                t = 2 * (q % 2) + e
+                add_self_term(both[:, t, 1, :, :], both[:, t, 0, :, :], banks[e])
+            o = rows.tile([P, 2, 4 * D], F32, name="o")
+            for e, copy in enumerate([scalar_copy, second_copy]):
                 copy(
-                    ilv[e],
-                    o[:, e, :].rearrange("p (f j) -> p f j", j=2),
-                    tl[:, t, :, :, :].rearrange("p j c s -> p (c s) j"),
+                    o[:, e, :].rearrange("p (ds j) -> p ds j", j=2),
+                    both[:, 2 * (q % 2) + e, :, :, :].rearrange("p j d s -> p (d s) j"),
                 )
-                if split:
-                    nc.sync.dma_start(
-                        out=out[b, 256 * gu : 256 * (gu + 1)].rearrange("(p e) l f -> p e (l f)", e=2)[:, e, :],
-                        in_=o[:, e, :],
-                    )
-            if not split:
-                nc.sync.dma_start(
-                    out=out[b, 256 * gu : 256 * (gu + 1)].rearrange("(p e) l f -> p (e l f)", e=2),
-                    in_=o[:].rearrange("p e f -> p (e f)"),
-                )
+            nc.sync.dma_start(
+                out=out[b, 256 * q : 256 * (q + 1)].rearrange("(p e) l hk -> p (e l hk)", e=2),
+                in_=o[:].rearrange("p e dk -> p (e dk)"),
+            )
 
-        for b in range(X_FIRST):
-            regroup_x(b)
-            quant_x(b)
-        bank_of = {}
-
-        def mm(nts):
-            for nt in nts:
-                bank_of[nt] = hop1_mm(0, nt)
-
-        def add(nts):
-            for nt in nts:
-                hop1_add(0, nt, bank_of[nt])
-
-        for gu in range(2):
+        quantise_x(0, vector_copy)
+        for q in range(QUARTERS):
             for s in range(S):
-                transpose_a(s, gu, E_ENG[2 * gu + s])
-                quant_a(s, gu)
-        mm([0, 1])
-        transpose_a(0, 2, E_ENG[4])
-        transpose_a(1, 2, E_ENG[5])
-        add([0, 1])
-        quant_a(0, 2)
-        quant_a(1, 2)
-        mm([2])
-        transpose_a(0, 3, E_ENG[6])
-        transpose_a(1, 3, E_ENG[7])
-        if X_FIRST < 2:
-            regroup_x(1)
-        add([2])
-        mm([3, 4, 5])
-        add([3])
-        grp00 = regroup_h(0, 0, R_ENG[0])
-        quant_a(0, 3)
-        add([4])
-        quant_a(1, 3)
-        add([5])
-        mm([6, 7])
-        add([6, 7])
-        grp01 = regroup_h(0, 1, R_ENG[1])
-        quant_h(0, 0, grp00)
-        if X_FIRST < 2:
-            quant_x(1)
-        quant_h(0, 1, grp01)
-        if X_FIRST < 3 and XR2_AT < 0:
-            regroup_x(2)
-
-        ones = [(b, gu) for b in range(1, B) for gu in range(4)]
-        twos = [(b, gu) for b in range(B) for gu in range(4)]
-        for b, gu in ones[:PRE]:
-            hop1_unit(b, gu)
-        ones = ones[PRE:]
-        for i, (b, gu) in enumerate(twos):
-            hop2_unit(b, gu, ILV[i], i >= len(twos) - SPLIT_STORES)
-            if i == XR2_AT and X_FIRST < 3:
-                regroup_x(2)
-            if i == XR3_AT and X_FIRST < 4:
-                regroup_x(3)
-            if i == XQ2_AT and X_FIRST < 3:
-                quant_x(2)
-            if i == XQ3_AT and X_FIRST < 4:
-                quant_x(3)
-            for b1, gu1 in ones[: RATES[i]]:
-                hop1_unit(b1, gu1)
-            ones = ones[RATES[i] :]
+                quantise_a(s, q)
+            if q >= 1:
+                hop1(0, q - 1)
+        hop1(0, QUARTERS - 1)
+        first_hop = [(b, q) for b in range(1, B) for q in range(QUARTERS)]
+        second_hop = [(b, q) for b in range(B) for q in range(QUARTERS)]
+        for b, q in first_hop[:LEAD]:
+            hop1(b, q)
+        for i, (b, q) in enumerate(second_hop):
+            hop2(b, q, vector_copy if i == len(second_hop) - 1 else gpsimd_copy)
+            if i + LEAD < len(first_hop):
+                hop1(*first_hop[i + LEAD])

@@ -18,19 +18,17 @@ S = 2
 QUARTERS = 4
 FLOPS = 4 * 2 * 1024 * 1024 * 1024
 
-LEAD = 1
-
 
 def tile_ginconvfft_pa_t_kernel(tc, x, support, eps, out):
     nc = tc.nc
     with ExitStack() as ctx:
         keep = ctx.enter_context(tc.tile_pool(name="keep", bufs=1))
-        at_stage = ctx.enter_context(tc.tile_pool(name="at_stage", bufs=4))
-        x_stage = ctx.enter_context(tc.tile_pool(name="x_stage", bufs=2))
-        h_stage = ctx.enter_context(tc.tile_pool(name="h_stage", bufs=3))
-        big = ctx.enter_context(tc.tile_pool(name="big", bufs=6))
-        h_mx = ctx.enter_context(tc.tile_pool(name="h_mx", bufs=6))
-        rows = ctx.enter_context(tc.tile_pool(name="rows", bufs=4))
+        at_stage = ctx.enter_context(tc.tile_pool(name="atg", bufs=4))
+        x_stage = ctx.enter_context(tc.tile_pool(name="xg", bufs=2))
+        big = ctx.enter_context(tc.tile_pool(name="hh", bufs=6))
+        h_stage = ctx.enter_context(tc.tile_pool(name="hg", bufs=3))
+        h_mx = ctx.enter_context(tc.tile_pool(name="hc", bufs=6))
+        rows = ctx.enter_context(tc.tile_pool(name="o", bufs=4))
         psum = ctx.enter_context(tc.psum_pool(name="psum", bufs=8))
 
         def vector_copy(dst, src):
@@ -44,21 +42,21 @@ def tile_ginconvfft_pa_t_kernel(tc, x, support, eps, out):
 
         ident = keep.tile([P, P], F32, name="ident")
         make_identity(nc, ident[:])
-
         eps_row = keep.tile([P, 32], BF16, name="eps_row")
         nc.vector.memset(eps_row[:], 0.0)
         ones = keep.tile([P, P], BF16, name="ones")
         nc.vector.memset(ones[:], 1.0)
         nc.scalar.dma_start(out=eps_row[0:1, 0:1], in_=eps.rearrange("(o n) -> o n", o=1))
-        eps_bank = psum.tile([P, 512], F32, name="bank")
+        eps_bank = psum.tile([P, 512], F32, name="bank", tag="bank")
         nc.tensor.matmul(out=eps_bank[:, 0:32], lhsT=ones[:], rhs=eps_row[:], start=True, stop=True)
         gain = keep.tile([P, 1], F32, name="gain")
         nc.vector.tensor_scalar_add(out=gain[:], in0=eps_bank[:, 0:1], scalar1=1.0)
 
-        x_raw = [keep.tile([P, 2 * QUARTERS, D], BF16, name="x_raw%d" % b) for b in range(B)]
-        a_raw = [big.tile([P, 4, 2048], BF16, name="a_raw", tag="big") for half in range(2)]
+        x_raw = {}
+        a_raw = {}
 
         def load_x(b):
+            x_raw[b] = keep.tile([P, 2 * QUARTERS, D], BF16, name="x_raw%d" % b)
             nc.sync.dma_start(
                 out=x_raw[b][:].rearrange("p (q e) d -> p q (e d)", e=2),
                 in_=x[b].rearrange("(q p e) l h -> p q (e l h)", q=QUARTERS, p=P, e=2),
@@ -66,6 +64,8 @@ def tile_ginconvfft_pa_t_kernel(tc, x, support, eps, out):
 
         load_x(0)
         for q in range(QUARTERS):
+            if q % 2 == 0:
+                a_raw[q // 2] = big.tile([P, 4, 2048], BF16, name="a_raw", tag="hh")
             for s in range(S):
                 nc.sync.dma_start(
                     out=a_raw[q // 2][:, 2 * (q % 2) + s, :],
@@ -74,30 +74,35 @@ def tile_ginconvfft_pa_t_kernel(tc, x, support, eps, out):
         for b in range(1, B):
             load_x(b)
 
+        x_grouped = {}
         x_codes = {}
         x_scales = {}
 
-        def quantise_x(b, copy):
-            grouped = x_stage.tile([P, 2, D, 4], BF16, name="x_grouped", align_bytes=64)
+        def regroup_x(b, copy):
+            x_grouped[b] = x_stage.tile([P, 2, D, 4], BF16, name="x_grp", align_bytes=64)
             for g in range(2):
-                copy(grouped[:, g, :, :], x_raw[b][:, 4 * g : 4 * (g + 1), :].rearrange("p t d -> p d t"))
+                copy(x_grouped[b][:, g, :, :], x_raw[b][:, 4 * g : 4 * (g + 1), :].rearrange("p t d -> p d t"))
+
+        def quantise_x(b):
             x_codes[b] = keep.tile([P, 2 * D], U32, name="x_codes%d" % b, align_bytes=64)
             x_scales[b] = keep.tile([P, 2 * D], U8, name="x_scales%d" % b, align_bytes=64)
             nc.vector.quantize_mx(
                 out=x_codes[b][:].bitcast(FP8X4),
                 scales=x_scales[b][:],
-                in_=grouped[:].rearrange("p g d t -> p (g d t)"),
+                in_=x_grouped[b][:].rearrange("p g d t -> p (g d t)"),
             )
 
+        at_grouped = {}
         at_codes = {}
         at_scales = {}
 
-        def quantise_a(s, q):
+        def transpose_a(s, q):
             words = a_raw[q // 2][:, 2 * (q % 2) + s, :].bitcast(F32)
-            grouped = at_stage.tile([P, 2048], BF16, name="at_grouped", align_bytes=64)
-            grouped_words = grouped[:].bitcast(F32)
+            at_grouped[(s, q)] = at_stage.tile([P, 2048], BF16, name="at_grp", align_bytes=64)
+            grouped_words = at_grouped[(s, q)][:].bitcast(F32)
+            banks = []
             for g in range(2):
-                bank = psum.tile([P, 512], F32, name="bank")
+                bank = psum.tile([P, 512], F32, name="bank", tag="bank")
                 for u in range(2):
                     for e in range(2):
                         first_word = 512 * e + 256 * g + 128 * u
@@ -106,16 +111,23 @@ def tile_ginconvfft_pa_t_kernel(tc, x, support, eps, out):
                             in_=words[:, first_word : first_word + 128],
                             identity=ident[:],
                         )
+                banks.append(bank)
+            for g in range(2):
                 scalar_copy(
                     grouped_words[:, 512 * g : 512 * (g + 1)].rearrange("p (col u) -> p col u", u=2),
-                    bank[:].rearrange("p (u col) -> p col u", u=2),
+                    banks[g][:].rearrange("p (u col) -> p col u", u=2),
                 )
+
+        def quantise_a(s, q):
             at_codes[(s, q)] = keep.tile([P, 512], U32, name="at_codes%d_%d" % (s, q), align_bytes=64)
             at_scales[(s, q)] = keep.tile([P, 512], U8, name="at_scales%d_%d" % (s, q), align_bytes=64)
-            nc.vector.quantize_mx(out=at_codes[(s, q)][:].bitcast(FP8X4), scales=at_scales[(s, q)][:], in_=grouped[:])
+            nc.vector.quantize_mx(
+                out=at_codes[(s, q)][:].bitcast(FP8X4), scales=at_scales[(s, q)][:], in_=at_grouped[(s, q)][:]
+            )
 
-        def products(q, e, moving):
-            bank = psum.tile([P, 512], F32, name="bank")
+        def products(tile_no, moving):
+            q, e = tile_no // 2, tile_no % 2
+            bank = psum.tile([P, 512], F32, name="bank", tag="bank")
             for s in range(S):
                 for g in range(2):
                     cols = slice(256 * g + 128 * e, 256 * g + 128 * (e + 1))
@@ -142,61 +154,62 @@ def tile_ginconvfft_pa_t_kernel(tc, x, support, eps, out):
             )
 
         h = {}
+        h_grouped = {}
         h_codes = {}
         h_scales = {}
 
-        def hop1(b, q):
-            if q == 0 and b + 1 < B:
-                quantise_x(b + 1, scalar_copy)
-            g = q // 2
-            banks = [
-                products(
-                    q,
-                    e,
-                    lambda s, pass_g: (
-                        x_codes[b][:, D * pass_g : D * (pass_g + 1)],
-                        x_scales[b][:, D * pass_g : D * (pass_g + 1)],
-                    ),
-                )
-                for e in range(2)
-            ]
-            if q % 2 == 0:
-                h[(b, g)] = big.tile([P, 4, 2, D, S], F32, name="h", tag="big")
-            for e in range(2):
-                add_self_term(
-                    h[(b, g)][:, 2 * (q % 2) + e, 0, :, :],
-                    x_raw[b][:, 2 * q + e, :].unsqueeze(2).to_broadcast([P, D, S]),
-                    banks[e],
-                )
-            if q % 2 == 1:
-                grouped = h_stage.tile([P, S, D, 4], BF16, name="h_grouped", align_bytes=64)
-                for s, copy in enumerate([scalar_copy, gpsimd_copy]):
-                    copy(grouped[:, s, :, :], h[(b, g)][:, :, 0, :, s].rearrange("p t d -> p d t"))
-                h_codes[(b, g)] = h_mx.tile([P, S * D], U32, name="h_codes", align_bytes=64)
-                h_scales[(b, g)] = h_mx.tile([P, S * D], U8, name="h_scales", align_bytes=64)
-                nc.vector.quantize_mx(
-                    out=h_codes[(b, g)][:].bitcast(FP8X4),
-                    scales=h_scales[(b, g)][:],
-                    in_=grouped[:].rearrange("p s d t -> p (s d t)"),
-                )
+        def hop1_products(b, tile_no):
+            return products(
+                tile_no,
+                lambda s, g: (x_codes[b][:, D * g : D * (g + 1)], x_scales[b][:, D * g : D * (g + 1)]),
+            )
 
-        def hop2(b, q, second_copy):
+        def hop1_add(b, tile_no, bank):
+            g, t = tile_no // 4, tile_no % 4
+            if t == 0:
+                h[(b, g)] = big.tile([P, 4, 2, D, S], F32, name="hh", tag="hh")
+            add_self_term(
+                h[(b, g)][:, t, 0, :, :],
+                x_raw[b][:, tile_no, :].unsqueeze(2).to_broadcast([P, D, S]),
+                bank,
+            )
+
+        def regroup_h(b, g):
+            h_grouped[(b, g)] = h_stage.tile([P, S, D, 4], BF16, name="h_grp", align_bytes=64)
+            for s, copy in enumerate([scalar_copy, scalar_copy if g == 0 else gpsimd_copy]):
+                copy(h_grouped[(b, g)][:, s, :, :], h[(b, g)][:, :, 0, :, s].rearrange("p t d -> p d t"))
+
+        def quantise_h(b, g):
+            h_codes[(b, g)] = h_mx.tile([P, S * D], U32, name="h_codes", align_bytes=64)
+            h_scales[(b, g)] = h_mx.tile([P, S * D], U8, name="h_scales", align_bytes=64)
+            nc.vector.quantize_mx(
+                out=h_codes[(b, g)][:].bitcast(FP8X4),
+                scales=h_scales[(b, g)][:],
+                in_=h_grouped[(b, g)][:].rearrange("p s d t -> p (s d t)"),
+            )
+
+        def hop1_unit(b, q):
+            banks = [hop1_products(b, 2 * q + e) for e in range(2)]
+            for e in range(2):
+                hop1_add(b, 2 * q + e, banks[e])
+            if q % 2 == 1:
+                regroup_h(b, q // 2)
+
+        def hop2_unit(b, q, second_copy, to_quantise):
             banks = [
                 products(
-                    q,
-                    e,
-                    lambda s, pass_g: (
-                        h_codes[(b, pass_g)][:, D * s : D * (s + 1)],
-                        h_scales[(b, pass_g)][:, D * s : D * (s + 1)],
-                    ),
+                    2 * q + e,
+                    lambda s, g: (h_codes[(b, g)][:, D * s : D * (s + 1)], h_scales[(b, g)][:, D * s : D * (s + 1)]),
                 )
                 for e in range(2)
             ]
+            o = rows.tile([P, 2, 4 * D], F32, name="o")
             both = h[(b, q // 2)]
             for e in range(2):
                 t = 2 * (q % 2) + e
                 add_self_term(both[:, t, 1, :, :], both[:, t, 0, :, :], banks[e])
-            o = rows.tile([P, 2, 4 * D], F32, name="o")
+            for b1, g1 in to_quantise:
+                quantise_h(b1, g1)
             for e, copy in enumerate([scalar_copy, second_copy]):
                 copy(
                     o[:, e, :].rearrange("p (ds j) -> p ds j", j=2),
@@ -207,18 +220,60 @@ def tile_ginconvfft_pa_t_kernel(tc, x, support, eps, out):
                 in_=o[:].rearrange("p e dk -> p (e dk)"),
             )
 
-        quantise_x(0, vector_copy)
-        for q in range(QUARTERS):
+        regroup_x(0, vector_copy)
+        quantise_x(0)
+        for q in range(2):
             for s in range(S):
+                transpose_a(s, q)
                 quantise_a(s, q)
-            if q >= 1:
-                hop1(0, q - 1)
-        hop1(0, QUARTERS - 1)
+        bank_of = {}
+        for tile_no in [0, 1]:
+            bank_of[tile_no] = hop1_products(0, tile_no)
+        for s in range(S):
+            transpose_a(s, 2)
+        for tile_no in [0, 1]:
+            hop1_add(0, tile_no, bank_of[tile_no])
+        for s in range(S):
+            quantise_a(s, 2)
+        bank_of[2] = hop1_products(0, 2)
+        for s in range(S):
+            transpose_a(s, 3)
+        regroup_x(1, scalar_copy)
+        hop1_add(0, 2, bank_of[2])
+        for tile_no in [3, 4, 5]:
+            bank_of[tile_no] = hop1_products(0, tile_no)
+        hop1_add(0, 3, bank_of[3])
+        regroup_h(0, 0)
+        quantise_a(0, 3)
+        hop1_add(0, 4, bank_of[4])
+        quantise_a(1, 3)
+        hop1_add(0, 5, bank_of[5])
+        for tile_no in [6, 7]:
+            bank_of[tile_no] = hop1_products(0, tile_no)
+        for tile_no in [6, 7]:
+            hop1_add(0, tile_no, bank_of[tile_no])
+        regroup_h(0, 1)
+        quantise_h(0, 0)
+        quantise_x(1)
+        quantise_h(0, 1)
+        regroup_x(2, scalar_copy)
+
         first_hop = [(b, q) for b in range(1, B) for q in range(QUARTERS)]
         second_hop = [(b, q) for b in range(B) for q in range(QUARTERS)]
-        for b, q in first_hop[:LEAD]:
-            hop1(b, q)
+        hop1_unit(*first_hop[0])
         for i, (b, q) in enumerate(second_hop):
-            hop2(b, q, vector_copy if i == len(second_hop) - 1 else gpsimd_copy)
-            if i + LEAD < len(first_hop):
-                hop1(*first_hop[i + LEAD])
+            b1, q1 = first_hop[min(i, len(first_hop) - 1)]
+            hop2_unit(
+                b,
+                q,
+                vector_copy if i == len(second_hop) - 1 else gpsimd_copy,
+                [(b1, q1 // 2)] if (i < len(first_hop) and q1 % 2 == 1) else [],
+            )
+            if i == 1:
+                regroup_x(3, scalar_copy)
+            if i == 0:
+                quantise_x(2)
+            if i == 3:
+                quantise_x(3)
+            if i + 1 < len(first_hop):
+                hop1_unit(*first_hop[i + 1])

from contextlib import ExitStack

import concourse.mybir as mybir
from concourse.masks import make_identity

F32 = mybir.dt.float32
BF16 = mybir.dt.bfloat16
U32 = mybir.dt.uint32
U8 = mybir.dt.uint8
FP8X4 = mybir.dt.float8_e4m3fn_x4
MULT = mybir.AluOpType.mult
ADD = mybir.AluOpType.add

P = 128
B = 4
D = 256
S = 2
QUARTERS = 4
FLOPS = 4 * 2 * 1024 * 1024 * 1024


def tile_ginconvfft_pa_t_kernel(tc, x, support, eps, out):
    nc = tc.nc
    with ExitStack() as ctx:
        keep = ctx.enter_context(tc.tile_pool(name="keep", bufs=1))
        at_stage = ctx.enter_context(tc.tile_pool(name="atg", bufs=4))
        x_stage = ctx.enter_context(tc.tile_pool(name="xg", bufs=2))
        big = ctx.enter_context(tc.tile_pool(name="hh", bufs=6))
        h_stage = ctx.enter_context(tc.tile_pool(name="hg", bufs=3))
        h_mx = ctx.enter_context(tc.tile_pool(name="hc", bufs=6))
        rows = ctx.enter_context(tc.tile_pool(name="o", bufs=4))
        psum = ctx.enter_context(tc.psum_pool(name="psum", bufs=8))

        def vector_copy(dst, src):
            nc.vector.tensor_copy(out=dst, in_=src)

        def scalar_copy(dst, src):
            nc.scalar.copy(out=dst, in_=src)

        def gpsimd_copy(dst, src):
            nc.gpsimd.tensor_scalar(out=dst, in0=src, scalar1=1.0, scalar2=0.0, op0=MULT, op1=ADD)

        ident = keep.tile([P, P], F32, name="ident")
        make_identity(nc, ident[:])
        eps_row = keep.tile([P, 32], BF16, name="eps_row")
        nc.vector.memset(eps_row[:], 0.0)
        ones = keep.tile([P, P], BF16, name="ones")
        nc.vector.memset(ones[:], 1.0)
        nc.scalar.dma_start(out=eps_row[0:1, 0:1], in_=eps.rearrange("(o n) -> o n", o=1))
        eps_bank = psum.tile([P, 512], F32, name="bank", tag="bank")
        nc.tensor.matmul(out=eps_bank[:, 0:32], lhsT=ones[:], rhs=eps_row[:], start=True, stop=True)
        gain = keep.tile([P, 1], F32, name="gain")
        nc.vector.tensor_scalar_add(out=gain[:], in0=eps_bank[:, 0:1], scalar1=1.0)

        x_raw = {}
        a_raw = {}

        def load_x(b):
            x_raw[b] = keep.tile([P, 2 * QUARTERS, D], BF16, name="x_raw%d" % b)
            nc.sync.dma_start(
                out=x_raw[b][:].rearrange("p (q e) d -> p q (e d)", e=2),
                in_=x[b].rearrange("(q p e) l h -> p q (e l h)", q=QUARTERS, p=P, e=2),
            )

        load_x(0)
        for q in range(QUARTERS):
            if q % 2 == 0:
                a_raw[q // 2] = big.tile([P, 4, 2048], BF16, name="a_raw", tag="hh")
            for s in range(S):
                nc.sync.dma_start(
                    out=a_raw[q // 2][:, 2 * (q % 2) + s, :],
                    in_=support[s, 256 * q : 256 * (q + 1), :].rearrange("(p e) m -> p (e m)", e=2),
                )
        for b in range(1, B):
            load_x(b)

        x_grouped = {}
        x_codes = {}
        x_scales = {}

        def regroup_x(b, copy):
            x_grouped[b] = x_stage.tile([P, 2, D, 4], BF16, name="x_grp", align_bytes=64)
            for g in range(2):
                copy(x_grouped[b][:, g, :, :], x_raw[b][:, 4 * g : 4 * (g + 1), :].rearrange("p t d -> p d t"))

        def quantise_x(b):
            x_codes[b] = keep.tile([P, 2 * D], U32, name="x_codes%d" % b, align_bytes=64)
            x_scales[b] = keep.tile([P, 2 * D], U8, name="x_scales%d" % b, align_bytes=64)
            nc.vector.quantize_mx(
                out=x_codes[b][:].bitcast(FP8X4),
                scales=x_scales[b][:],
                in_=x_grouped[b][:].rearrange("p g d t -> p (g d t)"),
            )

        at_grouped = {}
        at_codes = {}
        at_scales = {}

        def transpose_a(s, q):
            words = a_raw[q // 2][:, 2 * (q % 2) + s, :].bitcast(F32)
            at_grouped[(s, q)] = at_stage.tile([P, 2048], BF16, name="at_grp", align_bytes=64)
            grouped_words = at_grouped[(s, q)][:].bitcast(F32)
            banks = []
            for g in range(2):
                bank = psum.tile([P, 512], F32, name="bank", tag="bank")
                for u in range(2):
                    for e in range(2):
                        first_word = 512 * e + 256 * g + 128 * u
                        nc.tensor.transpose(
                            out=bank[:, 256 * u + 128 * e : 256 * u + 128 * (e + 1)],
                            in_=words[:, first_word : first_word + 128],
                            identity=ident[:],
                        )
                banks.append(bank)
            for g in range(2):
                scalar_copy(
                    grouped_words[:, 512 * g : 512 * (g + 1)].rearrange("p (col u) -> p col u", u=2),
                    banks[g][:].rearrange("p (u col) -> p col u", u=2),
                )

        def quantise_a(s, q):
            at_codes[(s, q)] = keep.tile([P, 512], U32, name="at_codes%d_%d" % (s, q), align_bytes=64)
            at_scales[(s, q)] = keep.tile([P, 512], U8, name="at_scales%d_%d" % (s, q), align_bytes=64)
            nc.vector.quantize_mx(
                out=at_codes[(s, q)][:].bitcast(FP8X4), scales=at_scales[(s, q)][:], in_=at_grouped[(s, q)][:]
            )

        def products(tile_no, moving):
            q, e = tile_no // 2, tile_no % 2
            bank = psum.tile([P, 512], F32, name="bank", tag="bank")
            for s in range(S):
                for g in range(2):
                    cols = slice(256 * g + 128 * e, 256 * g + 128 * (e + 1))
                    codes, scales = moving(s, g)
                    nc.tensor.matmul_mx(
                        out=bank[:, D * s : D * (s + 1)],
                        lhsT=at_codes[(s, q)][:, cols].bitcast(FP8X4),
                        lhsT_scale=at_scales[(s, q)][:, cols],
                        rhs=codes.bitcast(FP8X4),
                        rhs_scale=scales,
                        start=(g == 0),
                        stop=(g == 1),
                    )
            return bank

        def add_self_term(dst, previous, bank):
            nc.vector.scalar_tensor_tensor(
                out=dst,
                in0=previous,
                scalar=gain[:, 0:1],
                in1=bank[:].rearrange("p (s d) -> p d s", s=S),
                op0=MULT,
                op1=ADD,
            )

        h = {}
        h_grouped = {}
        h_codes = {}
        h_scales = {}

        def hop1_products(b, tile_no):
            return products(
                tile_no,
                lambda s, g: (x_codes[b][:, D * g : D * (g + 1)], x_scales[b][:, D * g : D * (g + 1)]),
            )

        def hop1_add(b, tile_no, bank):
            g, t = tile_no // 4, tile_no % 4
            if t == 0:
                h[(b, g)] = big.tile([P, 4, 2, D, S], F32, name="hh", tag="hh")
            add_self_term(
                h[(b, g)][:, t, 0, :, :],
                x_raw[b][:, tile_no, :].unsqueeze(2).to_broadcast([P, D, S]),
                bank,
            )

        def regroup_h(b, g):
            h_grouped[(b, g)] = h_stage.tile([P, S, D, 4], BF16, name="h_grp", align_bytes=64)
            for s, copy in enumerate([scalar_copy, scalar_copy if g == 0 else gpsimd_copy]):
                copy(h_grouped[(b, g)][:, s, :, :], h[(b, g)][:, :, 0, :, s].rearrange("p t d -> p d t"))

        def quantise_h(b, g):
            h_codes[(b, g)] = h_mx.tile([P, S * D], U32, name="h_codes", align_bytes=64)
            h_scales[(b, g)] = h_mx.tile([P, S * D], U8, name="h_scales", align_bytes=64)
            nc.vector.quantize_mx(
                out=h_codes[(b, g)][:].bitcast(FP8X4),
                scales=h_scales[(b, g)][:],
                in_=h_grouped[(b, g)][:].rearrange("p s d t -> p (s d t)"),
            )

        def hop1_unit(b, q):
            banks = [hop1_products(b, 2 * q + e) for e in range(2)]
            for e in range(2):
                hop1_add(b, 2 * q + e, banks[e])
            if q % 2 == 1:
                regroup_h(b, q // 2)

        def hop2_unit(b, q, second_copy, to_quantise):
            banks = [
                products(
                    2 * q + e,
                    lambda s, g: (h_codes[(b, g)][:, D * s : D * (s + 1)], h_scales[(b, g)][:, D * s : D * (s + 1)]),
                )
                for e in range(2)
            ]
            o = rows.tile([P, 2, 4 * D], F32, name="o")
            both = h[(b, q // 2)]
            for e in range(2):
                t = 2 * (q % 2) + e
                add_self_term(both[:, t, 1, :, :], both[:, t, 0, :, :], banks[e])
            for b1, g1 in to_quantise:
                quantise_h(b1, g1)
            for e, copy in enumerate([scalar_copy, second_copy]):
                copy(
                    o[:, e, :].rearrange("p (ds j) -> p ds j", j=2),
                    both[:, 2 * (q % 2) + e, :, :, :].rearrange("p j d s -> p (d s) j"),
                )
            nc.sync.dma_start(
                out=out[b, 256 * q : 256 * (q + 1)].rearrange("(p e) l hk -> p (e l hk)", e=2),
                in_=o[:].rearrange("p e dk -> p (e dk)"),
            )

        regroup_x(0, vector_copy)
        quantise_x(0)
        for q in range(2):
            for s in range(S):
                transpose_a(s, q)
                quantise_a(s, q)
        bank_of = {}
        for tile_no in [0, 1]:
            bank_of[tile_no] = hop1_products(0, tile_no)
        for s in range(S):
            transpose_a(s, 2)
        for tile_no in [0, 1]:
            hop1_add(0, tile_no, bank_of[tile_no])
        for s in range(S):
            quantise_a(s, 2)
        bank_of[2] = hop1_products(0, 2)
        for s in range(S):
            transpose_a(s, 3)
        regroup_x(1, scalar_copy)
        hop1_add(0, 2, bank_of[2])
        for tile_no in [3, 4, 5]:
            bank_of[tile_no] = hop1_products(0, tile_no)
        hop1_add(0, 3, bank_of[3])
        regroup_h(0, 0)
        quantise_a(0, 3)
        hop1_add(0, 4, bank_of[4])
        quantise_a(1, 3)
        hop1_add(0, 5, bank_of[5])
        for tile_no in [6, 7]:
            bank_of[tile_no] = hop1_products(0, tile_no)
        for tile_no in [6, 7]:
            hop1_add(0, tile_no, bank_of[tile_no])
        regroup_h(0, 1)
        quantise_h(0, 0)
        quantise_x(1)
        quantise_h(0, 1)
        regroup_x(2, scalar_copy)

        first_hop = [(b, q) for b in range(1, B) for q in range(QUARTERS)]
        second_hop = [(b, q) for b in range(B) for q in range(QUARTERS)]
        hop1_unit(*first_hop[0])
        for i, (b, q) in enumerate(second_hop):
            b1, q1 = first_hop[min(i, len(first_hop) - 1)]
            hop2_unit(
                b,
                q,
                vector_copy if i == len(second_hop) - 1 else gpsimd_copy,
                [(b1, q1 // 2)] if (i < len(first_hop) and q1 % 2 == 1) else [],
            )
            if i == 1:
                regroup_x(3, scalar_copy)
            if i == 0:
                quantise_x(2)
            if i == 3:
                quantise_x(3)
            if i + 1 < len(first_hop):
                hop1_unit(*first_hop[i + 1])
